import numpy as np
import ml_dtypes


def mxq(x, axis, fmt="e4m3"):
    dtype, down = {"e4m3": (ml_dtypes.float8_e4m3fn, 7), "e5m2": (ml_dtypes.float8_e5m2, 14)}[fmt]
    v = np.moveaxis(np.asarray(x, np.float32).astype(ml_dtypes.bfloat16).astype(np.float64), axis, -1)
    blocks = v.reshape(v.shape[:-1] + (-1, 32))
    amax = np.abs(blocks).max(-1, keepdims=True)
    byte = np.maximum(np.where(amax > 0, np.frexp(amax)[1] - 1 + 127, 0) - down, 1)
    scale = np.exp2(byte - 127.0)
    codes = (blocks / scale).astype(np.float32).astype(dtype).astype(np.float64)
    return np.moveaxis((codes * scale).reshape(v.shape), -1, axis)


WIDE = False


def mx_kscale(k):
    if not WIDE:
        return np.ones(k)
    levels = np.array([10, -10, 5, -5, 0])
    a = np.random.permutation(np.resize(levels, k // 512 * 4)).reshape(k // 512, 4)
    idx = np.arange(k)
    return np.exp2(a[idx // 512, idx % 128 // 32])


BF16 = ml_dtypes.bfloat16


def bf(x):
    return np.asarray(x, np.float32).astype(BF16)


def f64(x):
    return np.asarray(x).astype(np.float64)


B, C, HH, WW, M, L, G, HID = 16, 512, 32, 32, 128, 512, 256, 512
N = HH * WW
ITERS = 3
DUST = 1.0


def lse(a, axis):
    top = a.max(axis=axis, keepdims=True)
    return np.log(np.exp(a - top).sum(axis=axis)) + np.squeeze(top, axis=axis)


def setup_inputs():
    s, t = mx_kscale(C), mx_kscale(HID)
    return {
        "x": bf(np.random.standard_normal((B, C, HH, WW)) * s[None, :, None, None]),
        "Ws1": bf(np.random.standard_normal((HID, C)) / np.sqrt(C) / s[None, :] * t[:, None]),
        "bs1": bf(np.random.standard_normal(HID) * 0.3 * t),
        "Ws2": bf(np.random.standard_normal((M, HID)) * 2.0 / np.sqrt(HID) / t[None, :]),
    }


def reference(x, Ws1, bs1, Ws2):
    xf = f64(x).reshape(B, C, N)
    hs = np.maximum((mxq(f64(Ws1), 1, "e4m3") @ mxq(xf, 1, "e4m3")) + f64(bs1)[None, :, None], 0.0)
    p = mxq(f64(Ws2), 1, "e4m3") @ mxq(hs, 1, "e4m3")
    norm = -np.log(M + N)
    log_mu = np.concatenate([np.full(M, norm), np.full(1, np.log(N) + norm)])
    log_nu = np.full(N, norm)
    Z = np.concatenate([p, np.full((B, 1, N), DUST)], axis=1)
    u = np.zeros((B, M + 1))
    v = np.zeros((B, N))
    for _ in range(ITERS):
        u = log_mu[None] - lse(Z + v[:, None, :], 2)
        v = log_nu[None] - lse(Z + u[:, :, None], 1)
    return np.exp(Z + u[:, :, None] + v[:, None, :] - norm)[:, :-1, :]

@@ -1,0 +1,364 @@
+import concourse.mybir as mybir
+from concourse.masks import make_identity
+
+F32 = mybir.dt.float32
+BF16 = mybir.dt.bfloat16
+U32 = mybir.dt.uint32
+U8 = mybir.dt.uint8
+FP8X4 = mybir.dt.float8_e4m3fn_x4
+ACT = mybir.ActivationFunctionType
+ALU = mybir.AluOpType
+AX = mybir.AxisListType
+
+P = 128
+PACK = 4
+IMAGES = 16
+CHANNELS = 512
+HIDDEN = 512
+CLUSTERS = 128
+PIXELS = 1024
+BANK = 512
+HALVES = PIXELS // BANK
+CHUNKS = PIXELS // P
+CHUNKS_PER_BANK = BANK // P
+ROUNDS = 3
+RUN = 4
+REPEAT = 16
+
+FLOPS = 2 * IMAGES * PIXELS * (CHANNELS * HIDDEN + HIDDEN * CLUSTERS)
+
+
+def tile_salad_pa_t_kernel(tc, x, Ws1, bs1, Ws2, out):
+    nc = tc.nc
+    with (
+        tc.tile_pool(name="consts", bufs=1) as consts,
+        tc.tile_pool(name="xs", bufs=2) as xs,
+        tc.tile_pool(name="hs", bufs=2) as hs,
+        tc.tile_pool(name="sk", bufs=5) as sk,
+        tc.tile_pool(name="small", bufs=4) as small,
+        tc.psum_pool(name="psum_z", bufs=2) as psum_z,
+        tc.psum_pool(name="psum_p", bufs=2) as psum_p,
+        tc.psum_pool(name="psum_t", bufs=3) as psum_t,
+        tc.psum_pool(name="psum_v", bufs=1) as psum_v,
+        tc.manual_schedule(),
+    ):
+        ident = consts.tile([P, P], F32)
+        make_identity(nc, ident[:])
+        mean_ones = consts.tile([P, P], F32)
+        nc.vector.memset(mean_ones[:], 1.0 / PIXELS)
+
+        w1_raw = consts.tile([P, PACK * CHANNELS], BF16)
+        nc.sync.dma_start(out=w1_raw[:], in_=Ws1.rearrange("(p t) c -> p (t c)", t=PACK))
+        w2_raw = consts.tile([P, HIDDEN], BF16)
+        nc.sync.dma_start(out=w2_raw[:], in_=Ws2)
+        bias_bf = consts.tile([P, PACK], BF16)
+        nc.sync.dma_start(out=bias_bf[:], in_=bs1.rearrange("(p t) -> p t", t=PACK))
+        bias = consts.tile([P, PACK], F32)
+        nc.vector.tensor_copy(out=bias[:], in_=bias_bf[:])
+
+        w1_grouped = consts.tile([P, PACK * P * PACK], BF16, align_bytes=64)
+        w2_grouped = consts.tile([P, P * PACK], BF16, align_bytes=64)
+        w1_codes = consts.tile([P, PACK * P], U32, align_bytes=64)
+        w1_scales = consts.tile([P, PACK * P], U8, align_bytes=64)
+        w2_codes = consts.tile([P, P], U32, align_bytes=64)
+        w2_scales = consts.tile([P, P], U8, align_bytes=64)
+
+        def group_weight_rows(rows, grouped):
+            words = rows.bitcast(F32).rearrange("p (q u) -> p u q", u=2)
+            flipped = psum_t.tile([P, CHUNKS_PER_BANK, P], F32, name="flipped", tag="flip")
+            for u in range(2):
+                nc.tensor.transpose(flipped[:, u, :], words[:, u, :], ident[:])
+            nc.vector.tensor_copy(
+                out=grouped.bitcast(F32).rearrange("p (r u) -> p r u", u=2),
+                in_=flipped[:, 0:2, :].rearrange("p u r -> p r u"),
+            )
+
+        for t in range(PACK):
+            group_weight_rows(
+                w1_raw[:, t * CHANNELS : (t + 1) * CHANNELS],
+                w1_grouped[:, t * P * PACK : (t + 1) * P * PACK],
+            )
+        group_weight_rows(w2_raw[:], w2_grouped[:])
+        nc.vector.quantize_mx(out=w1_codes[:].bitcast(FP8X4), scales=w1_scales[:], in_=w1_grouped[:])
+        nc.vector.quantize_mx(out=w2_codes[:].bitcast(FP8X4), scales=w2_scales[:], in_=w2_grouped[:])
+
+        x_raw, x_grouped, x_codes, x_scales = {}, {}, {}, {}
+        hs_planes, hs_grouped, hs_codes, hs_scales = {}, {}, {}, {}
+        scores, neg_tops, row_sum2s = {}, {}, {}
+        kern, kern_t, scaled_t = {}, {}, {}
+        scalings, sums, betas, beta_sums = {}, {}, {}, {}
+
+        def is_image(b):
+            return 0 <= b < IMAGES
+
+        def half_cols(half):
+            return slice(half * BANK, (half + 1) * BANK)
+
+        def regroup(dst, src):
+            nc.vector.tensor_copy(
+                out=dst.rearrange("p (c i) j -> p c j i", i=RUN),
+                in_=src.rearrange("p j (c i) -> p c j i", i=RUN),
+            )
+
+        def scaling_tile(step):
+            if step not in scalings:
+                fresh = small.tile([P, 2, ROUNDS], F32, name="scaling", tag="scaling")
+                nc.gpsimd.memset(fresh[:], 1.0)
+                scalings[step] = fresh
+            return scalings[step]
+
+        def load_image(b):
+            if not is_image(b):
+                return
+            x_raw[b] = xs.tile([P, PACK, PIXELS], BF16, name="x_raw", tag="x_raw", bufs=3)
+            nc.sync.dma_start(out=x_raw[b][:], in_=x[b].rearrange("(p j) h w -> p j (h w)", j=PACK))
+
+        def regroup_image(b):
+            if not is_image(b):
+                return
+            x_grouped[b] = xs.tile([P, PIXELS, PACK], BF16, name="x_grouped", tag="x_grouped", align_bytes=64)
+            regroup(x_grouped[b][:], x_raw[b][:])
+
+        def quantise_image(b):
+            if not is_image(b):
+                return
+            x_codes[b] = xs.tile([P, PIXELS], U32, name="x_codes", tag="x_codes", align_bytes=64)
+            x_scales[b] = xs.tile([P, PIXELS], U8, name="x_scales", tag="x_scales", align_bytes=64)
+            nc.vector.quantize_mx(
+                out=x_codes[b][:].bitcast(FP8X4),
+                scales=x_scales[b][:],
+                in_=x_grouped[b][:].rearrange("p n j -> p (n j)"),
+            )
+
+        def hidden_pass(b, k):
+            if not is_image(b):
+                return
+            half, t = divmod(k, PACK)
+            if k == 0:
+                hs_planes[b] = hs.tile([P, PACK, PIXELS], BF16, name="hs_planes", tag="hs_planes")
+            rows = slice(t * P, (t + 1) * P)
+            z = psum_z.tile([P, BANK], F32, name="z", tag="z")
+            nc.tensor.matmul_mx(
+                out=z[:],
+                lhsT=w1_codes[:, rows].bitcast(FP8X4),
+                lhsT_scale=w1_scales[:, rows],
+                rhs=x_codes[b][:, half_cols(half)].bitcast(FP8X4),
+                rhs_scale=x_scales[b][:, half_cols(half)],
+                start=True,
+                stop=True,
+            )
+            nc.scalar.activation(
+                out=hs_planes[b][:, t, half_cols(half)], in_=z[:], func=ACT.Relu, bias=bias[:, t : t + 1], scale=1.0
+            )
+
+        def regroup_hidden(b, half):
+            if not is_image(b):
+                return
+            if half == 0:
+                hs_grouped[b] = hs.tile([P, PIXELS, PACK], BF16, name="hs_grouped", tag="hs_grouped", align_bytes=64)
+            regroup(hs_grouped[b][:, half_cols(half), :], hs_planes[b][:, :, half_cols(half)])
+
+        def quantise_hidden(b, half):
+            if not is_image(b):
+                return
+            if half == 0:
+                hs_codes[b] = hs.tile([P, PIXELS], U32, name="hs_codes", tag="hs_codes", align_bytes=64)
+                hs_scales[b] = hs.tile([P, PIXELS], U8, name="hs_scales", tag="hs_scales", align_bytes=64)
+            nc.vector.quantize_mx(
+                out=hs_codes[b][:, half_cols(half)].bitcast(FP8X4),
+                scales=hs_scales[b][:, half_cols(half)],
+                in_=hs_grouped[b][:, half_cols(half), :].rearrange("p n j -> p (n j)"),
+            )
+
+        def cluster_scores(b):
+            if not is_image(b):
+                return
+            scores[b] = []
+            for half in range(HALVES):
+                score = psum_p.tile([P, BANK], F32, name="score", tag="score")
+                nc.tensor.matmul_mx(
+                    out=score[:],
+                    lhsT=w2_codes[:].bitcast(FP8X4),
+                    lhsT_scale=w2_scales[:],
+                    rhs=hs_codes[b][:, half_cols(half)].bitcast(FP8X4),
+                    rhs_scale=hs_scales[b][:, half_cols(half)],
+                    start=True,
+                    stop=True,
+                )
+                scores[b].append(score)
+
+        def row_tops(b):
+            if not is_image(b):
+                return
+            top2 = small.tile([P, HALVES], F32, name="top2", tag="top2")
+            for half in range(HALVES):
+                nc.vector.reduce_max(out=top2[:, half : half + 1], in_=scores[b][half][:], axis=AX.X)
+            neg_tops[b] = small.tile([P, 1], F32, name="neg_top", tag="neg_top")
+            nc.vector.tensor_scalar(
+                out=neg_tops[b][:], in0=top2[:, 0:1], scalar1=top2[:, 1:2], scalar2=-1.0, op0=ALU.max, op1=ALU.mult
+            )
+
+        def exponentials(b):
+            if not is_image(b):
+                return
+            kern[b] = sk.tile([P, PIXELS], F32, name="kern", tag="kern")
+            row_sum2s[b] = small.tile([P, HALVES], F32, name="row_sum2", tag="row_sum2")
+            for half in range(HALVES):
+                nc.scalar.activation(
+                    out=kern[b][:, half_cols(half)],
+                    in_=scores[b][half][:],
+                    func=ACT.Exp,
+                    bias=neg_tops[b][:, 0:1],
+                    scale=1.0,
+                    accum_out=row_sum2s[b][:, half : half + 1],
+                )
+
+        def first_alpha(b):
+            if not is_image(b):
+                return
+            row_sum = small.tile([P, 1], F32, name="row_sum", tag="row_sum")
+            nc.vector.reduce_sum(out=row_sum[:], in_=row_sum2s[b][:], axis=AX.X)
+            nc.vector.reciprocal(out=scaling_tile(b)[:, 0, 0:1], in_=row_sum[:])
+
+        def flip_kernel(b):
+            if not is_image(b):
+                return
+            kern_t[b] = sk.tile([P, CHUNKS, P], F32, name="kern_t", tag="kern_t")
+            for half in range(HALVES):
+                flipped = psum_t.tile([P, CHUNKS_PER_BANK, P], F32, name="flipped", tag="flip")
+                for q in range(CHUNKS_PER_BANK):
+                    j = half * CHUNKS_PER_BANK + q
+                    nc.tensor.transpose(flipped[:, q, :], kern[b][:, j * P : (j + 1) * P], ident[:])
+                nc.scalar.copy(
+                    out=kern_t[b][:, half * CHUNKS_PER_BANK : (half + 1) * CHUNKS_PER_BANK, :], in_=flipped[:]
+                )
+
+        def slots_of(step, rounds):
+            return [r for r in range(rounds) if is_image(step - r)]
+
+        def column_sums(step, r):
+            if not is_image(step - r):
+                return
+            if step not in sums:
+                sums[step] = psum_v.tile([P, ROUNDS * CHUNKS + 2 * ROUNDS, REPEAT], F32, name="sums", tag="sums")
+            for j in range(CHUNKS):
+                nc.tensor.matmul(
+                    out=sums[step][:, r * CHUNKS + j, :],
+                    lhsT=kern[step - r][:, j * P : (j + 1) * P],
+                    rhs=scaling_tile(step)[:, 0, r : r + 1].to_broadcast([P, REPEAT]),
+                    start=True,
+                    stop=True,
+                )
+
+        def new_betas(step):
+            slots = slots_of(step, ROUNDS)
+            if not slots:
+                return
+            lo, hi = slots[0], slots[-1] + 1
+            betas[step] = small.tile([P, ROUNDS, CHUNKS], F32, name="beta", tag="beta")
+            beta = betas[step]
+            nc.vector.tensor_tensor(
+                out=beta[:, lo:hi, :],
+                in0=sums[step][:, 0 : ROUNDS * CHUNKS, 0].rearrange("p (r j) -> p r j", j=CHUNKS)[:, lo:hi, :],
+                in1=scaling_tile(step)[:, 1, lo:hi].unsqueeze(2).to_broadcast([P, hi - lo, CHUNKS]),
+                op=ALU.add,
+            )
+            nc.vector.reciprocal(out=beta[:, lo:hi, :], in_=beta[:, lo:hi, :])
+            slots = slots_of(step, ROUNDS - 1)
+            if slots:
+                lo, hi = slots[0], slots[-1] + 1
+                beta_sums[step] = small.tile([P, ROUNDS], F32, name="beta_sum", tag="beta_sum")
+                nc.vector.reduce_sum(out=beta_sums[step][:, lo:hi], in_=beta[:, lo:hi, :], axis=AX.X)
+
+        def row_sums(step, r):
+            if not is_image(step - r):
+                return
+            base = ROUNDS * CHUNKS
+            for j in range(CHUNKS):
+                nc.tensor.matmul(
+                    out=sums[step][:, base + r, :],
+                    lhsT=kern_t[step - r][:, j, :],
+                    rhs=betas[step][:, r, j : j + 1].to_broadcast([P, REPEAT]),
+                    start=(j == 0),
+                    stop=(j == CHUNKS - 1),
+                )
+            nc.tensor.matmul(
+                out=sums[step][:, base + ROUNDS + r, :],
+                lhsT=mean_ones[:],
+                rhs=beta_sums[step][:, r : r + 1].to_broadcast([P, REPEAT]),
+                start=True,
+                stop=True,
+            )
+
+        def new_alphas(step):
+            slots = slots_of(step, ROUNDS - 1)
+            if not slots:
+                return
+            lo, hi = slots[0], slots[-1] + 1
+            nc.vector.reciprocal(
+                out=scaling_tile(step + 1)[:, :, lo + 1 : hi + 1],
+                in_=sums[step][:, ROUNDS * CHUNKS :, 0].rearrange("p (k r) -> p k r", r=ROUNDS)[:, :, lo:hi],
+            )
+
+        def scale_columns(step):
+            b = step - (ROUNDS - 1)
+            if not is_image(b):
+                return
+            scaled_t[b] = sk.tile([P, CHUNKS, P], F32, name="scaled", tag="scaled", bufs=2)
+            nc.vector.tensor_tensor(
+                out=scaled_t[b][:],
+                in0=kern_t[b][:],
+                in1=betas[step][:, ROUNDS - 1, :].unsqueeze(2).to_broadcast([P, CHUNKS, P]),
+                op=ALU.mult,
+            )
+
+        def flip_back_and_store(step):
+            b = step - (ROUNDS - 1)
+            if not is_image(b):
+                return
+            result = sk.tile([P, PIXELS], F32, name="result", tag="result", bufs=2)
+            for half in range(HALVES):
+                back = psum_t.tile([P, CHUNKS_PER_BANK, P], F32, name="back", tag="flip")
+                for q in range(CHUNKS_PER_BANK):
+                    nc.tensor.transpose(back[:, q, :], scaled_t[b][:, half * CHUNKS_PER_BANK + q, :], ident[:])
+                nc.scalar.activation(
+                    out=result[:, half_cols(half)],
+                    in_=back[:].rearrange("p q n -> p (q n)"),
+                    func=ACT.Copy,
+                    scale=scaling_tile(step)[:, 0, ROUNDS - 1 : ROUNDS],
+                )
+            nc.scalar.dma_start(out=out[b], in_=result[:])
+
+        for s in range(IMAGES + 4 + ROUNDS - 1):
+            fresh, hidden, scored, step = s - 1, s - 2, s - 3, s - 4
+            load_image(s)
+            if is_image(scored):
+                scaling_tile(scored)
+            regroup_hidden(scored, 1)
+            regroup_image(fresh)
+            hidden_pass(hidden, 0)
+            column_sums(step, 0)
+            hidden_pass(hidden, 1)
+            column_sums(step, 1)
+            quantise_hidden(scored, 1)
+            hidden_pass(hidden, 2)
+            column_sums(step, 2)
+            new_betas(step)
+            hidden_pass(hidden, 3)
+            cluster_scores(scored)
+            scale_columns(step)
+            row_tops(scored)
+            hidden_pass(hidden, 4)
+            row_sums(step, 0)
+            hidden_pass(hidden, 5)
+            row_sums(step, 1)
+            exponentials(scored)
+            regroup_hidden(hidden, 0)
+            hidden_pass(hidden, 6)
+            flip_back_and_store(step)
+            quantise_image(fresh)
+            quantise_hidden(hidden, 0)
+            first_alpha(scored)
+            new_alphas(step)
+            hidden_pass(hidden, 7)
+            flip_kernel(scored)

@@ -23,7 +23,9 @@ CHUNKS = PIXELS // P
 CHUNKS_PER_BANK = BANK // P
 ROUNDS = 3
 RUN = 4
-REPEAT = 16
+PIECES = 4
+PIECE = PIXELS // PIECES
+BLOCK = 8
 
 FLOPS = 2 * IMAGES * PIXELS * (CHANNELS * HIDDEN + HIDDEN * CLUSTERS)
 
@@ -34,7 +36,7 @@ def tile_salad_pa_t_kernel(tc, x, Ws1, bs1, Ws2, out):
         tc.tile_pool(name="consts", bufs=1) as consts,
         tc.tile_pool(name="xs", bufs=2) as xs,
         tc.tile_pool(name="hs", bufs=2) as hs,
-        tc.tile_pool(name="sk", bufs=5) as sk,
+        tc.tile_pool(name="sk", bufs=2) as sk,
         tc.tile_pool(name="small", bufs=4) as small,
         tc.psum_pool(name="psum_z", bufs=2) as psum_z,
         tc.psum_pool(name="psum_p", bufs=2) as psum_p,
@@ -84,9 +86,9 @@ def tile_salad_pa_t_kernel(tc, x, Ws1, bs1, Ws2, out):
 
         x_raw, x_grouped, x_codes, x_scales = {}, {}, {}, {}
         hs_planes, hs_grouped, hs_codes, hs_scales = {}, {}, {}, {}
-        scores, neg_tops, row_sum2s = {}, {}, {}
-        kern, kern_t, scaled_t = {}, {}, {}
-        scalings, sums, betas, beta_sums = {}, {}, {}, {}
+        scores, neg_tops = {}, {}
+        kern, kern_lo = {}, {}
+        alphas, alpha_parts, row_accs, sums, betas, beta_sums, spread = {}, {}, {}, {}, {}, {}, {}
 
         def is_image(b):
             return 0 <= b < IMAGES
@@ -94,18 +96,11 @@ def tile_salad_pa_t_kernel(tc, x, Ws1, bs1, Ws2, out):
         def half_cols(half):
             return slice(half * BANK, (half + 1) * BANK)
 
-        def regroup(dst, src):
-            nc.vector.tensor_copy(
-                out=dst.rearrange("p (c i) j -> p c j i", i=RUN),
-                in_=src.rearrange("p j (c i) -> p c j i", i=RUN),
+        def regrouped(dst, src):
+            return (
+                dst.rearrange("p (c i) j -> p c j i", i=RUN),
+                src.rearrange("p j (c i) -> p c j i", i=RUN),
             )
-
-        def scaling_tile(step):
-            if step not in scalings:
-                fresh = small.tile([P, 2, ROUNDS], F32, name="scaling", tag="scaling")
-                nc.gpsimd.memset(fresh[:], 1.0)
-                scalings[step] = fresh
-            return scalings[step]
 
         def load_image(b):
             if not is_image(b):
@@ -113,21 +108,25 @@ def tile_salad_pa_t_kernel(tc, x, Ws1, bs1, Ws2, out):
             x_raw[b] = xs.tile([P, PACK, PIXELS], BF16, name="x_raw", tag="x_raw", bufs=3)
             nc.sync.dma_start(out=x_raw[b][:], in_=x[b].rearrange("(p j) h w -> p j (h w)", j=PACK))
 
-        def regroup_image(b):
+        def regroup_image(b, piece):
             if not is_image(b):
                 return
-            x_grouped[b] = xs.tile([P, PIXELS, PACK], BF16, name="x_grouped", tag="x_grouped", align_bytes=64)
-            regroup(x_grouped[b][:], x_raw[b][:])
+            if piece == 0:
+                x_grouped[b] = xs.tile([P, PIXELS, PACK], BF16, name="x_grouped", tag="x_grouped", align_bytes=64)
+            cols = slice(piece * PIECE, (piece + 1) * PIECE)
+            dst, src = regrouped(x_grouped[b][:, cols, :], x_raw[b][:, :, cols])
+            nc.scalar.copy(out=dst, in_=src)
 
-        def quantise_image(b):
+        def quantise_image(b, half):
             if not is_image(b):
                 return
-            x_codes[b] = xs.tile([P, PIXELS], U32, name="x_codes", tag="x_codes", align_bytes=64)
-            x_scales[b] = xs.tile([P, PIXELS], U8, name="x_scales", tag="x_scales", align_bytes=64)
+            if half == 0:
+                x_codes[b] = xs.tile([P, PIXELS], U32, name="x_codes", tag="x_codes", align_bytes=64)
+                x_scales[b] = xs.tile([P, PIXELS], U8, name="x_scales", tag="x_scales", align_bytes=64)
             nc.vector.quantize_mx(
-                out=x_codes[b][:].bitcast(FP8X4),
-                scales=x_scales[b][:],
-                in_=x_grouped[b][:].rearrange("p n j -> p (n j)"),
+                out=x_codes[b][:, half_cols(half)].bitcast(FP8X4),
+                scales=x_scales[b][:, half_cols(half)],
+                in_=x_grouped[b][:, half_cols(half), :].rearrange("p n j -> p (n j)"),
             )
 
         def hidden_pass(b, k):
@@ -156,7 +155,8 @@ def tile_salad_pa_t_kernel(tc, x, Ws1, bs1, Ws2, out):
                 return
             if half == 0:
                 hs_grouped[b] = hs.tile([P, PIXELS, PACK], BF16, name="hs_grouped", tag="hs_grouped", align_bytes=64)
-            regroup(hs_grouped[b][:, half_cols(half), :], hs_planes[b][:, :, half_cols(half)])
+            dst, src = regrouped(hs_grouped[b][:, half_cols(half), :], hs_planes[b][:, :, half_cols(half)])
+            nc.vector.tensor_copy(out=dst, in_=src)
 
         def quantise_hidden(b, half):
             if not is_image(b):
@@ -198,11 +198,15 @@ def tile_salad_pa_t_kernel(tc, x, Ws1, bs1, Ws2, out):
                 out=neg_tops[b][:], in0=top2[:, 0:1], scalar1=top2[:, 1:2], scalar2=-1.0, op0=ALU.max, op1=ALU.mult
             )
 
-        def exponentials(b):
+        def row_acc_tile(step):
+            if step not in row_accs:
+                row_accs[step] = small.tile([P, ROUNDS, BLOCK], F32, name="row_acc", tag="row_acc")
+            return row_accs[step]
+
+        def exponentials(b, step):
             if not is_image(b):
                 return
-            kern[b] = sk.tile([P, PIXELS], F32, name="kern", tag="kern")
-            row_sum2s[b] = small.tile([P, HALVES], F32, name="row_sum2", tag="row_sum2")
+            kern[b] = sk.tile([P, PIXELS], F32, name="kern", tag="kern", bufs=9)
             for half in range(HALVES):
                 nc.scalar.activation(
                     out=kern[b][:, half_cols(half)],
@@ -210,155 +214,192 @@ def tile_salad_pa_t_kernel(tc, x, Ws1, bs1, Ws2, out):
                     func=ACT.Exp,
                     bias=neg_tops[b][:, 0:1],
                     scale=1.0,
-                    accum_out=row_sum2s[b][:, half : half + 1],
+                    accum_out=row_acc_tile(step + 1)[:, 0, half : half + 1],
                 )
 
-        def first_alpha(b):
+        def high_parts(b):
+            return kern[b][:].bitcast(BF16).rearrange("p (n two) -> p two n", two=2)[:, 1, :]
+
+        def low_parts(b):
             if not is_image(b):
                 return
-            row_sum = small.tile([P, 1], F32, name="row_sum", tag="row_sum")
-            nc.vector.reduce_sum(out=row_sum[:], in_=row_sum2s[b][:], axis=AX.X)
-            nc.vector.reciprocal(out=scaling_tile(b)[:, 0, 0:1], in_=row_sum[:])
+            kern_lo[b] = sk.tile([P, PIXELS], BF16, name="kern_lo", tag="kern_lo", bufs=7)
+            nc.vector.tensor_tensor(out=kern_lo[b][:], in0=kern[b][:], in1=high_parts(b), op=ALU.subtract)
 
-        def flip_kernel(b):
-            if not is_image(b):
-                return
-            kern_t[b] = sk.tile([P, CHUNKS, P], F32, name="kern_t", tag="kern_t")
-            for half in range(HALVES):
-                flipped = psum_t.tile([P, CHUNKS_PER_BANK, P], F32, name="flipped", tag="flip")
-                for q in range(CHUNKS_PER_BANK):
-                    j = half * CHUNKS_PER_BANK + q
-                    nc.tensor.transpose(flipped[:, q, :], kern[b][:, j * P : (j + 1) * P], ident[:])
-                nc.scalar.copy(
-                    out=kern_t[b][:, half * CHUNKS_PER_BANK : (half + 1) * CHUNKS_PER_BANK, :], in_=flipped[:]
-                )
+        def column_image(step, r):
+            return step - 5 - 2 * r
 
-        def slots_of(step, rounds):
-            return [r for r in range(rounds) if is_image(step - r)]
+        def row_image(step, r):
+            return step - 6 - 2 * r
+
+        def slot_range(image_of, step, rounds):
+            slots = [r for r in range(rounds) if is_image(image_of(step, r))]
+            if not slots:
+                return 0, 0
+            return slots[0], slots[-1] + 1
+
+        def alpha_tile(step):
+            if step not in alphas:
+                alphas[step] = small.tile([P, 2, ROUNDS], F32, name="alpha", tag="alpha")
+                nc.gpsimd.memset(alphas[step][:], 1.0)
+            return alphas[step]
+
+        def sums_tile(step):
+            if step not in sums:
+                sums[step] = psum_v.tile([P, ROUNDS * CHUNKS * 2 + ROUNDS], F32, name="sums", tag="sums")
+            return sums[step]
 
         def column_sums(step, r):
-            if not is_image(step - r):
+            b = column_image(step, r)
+            if not is_image(b):
                 return
-            if step not in sums:
-                sums[step] = psum_v.tile([P, ROUNDS * CHUNKS + 2 * ROUNDS, REPEAT], F32, name="sums", tag="sums")
             for j in range(CHUNKS):
+                at = (r * CHUNKS + j) * 2
+                cols = slice(j * P, (j + 1) * P)
                 nc.tensor.matmul(
-                    out=sums[step][:, r * CHUNKS + j, :],
-                    lhsT=kern[step - r][:, j * P : (j + 1) * P],
-                    rhs=scaling_tile(step)[:, 0, r : r + 1].to_broadcast([P, REPEAT]),
+                    out=sums_tile(step)[:, at : at + 2],
+                    lhsT=high_parts(b)[:, cols],
+                    rhs=alpha_parts[step][:, r, :],
                     start=True,
+                    stop=False,
+                )
+                nc.tensor.matmul(
+                    out=sums_tile(step)[:, at : at + 2],
+                    lhsT=kern_lo[b][:, cols],
+                    rhs=alpha_parts[step][:, r, :],
+                    start=False,
                     stop=True,
                 )
 
         def new_betas(step):
-            slots = slots_of(step, ROUNDS)
-            if not slots:
+            lo, hi = slot_range(column_image, step, ROUNDS)
+            if lo == hi:
                 return
-            lo, hi = slots[0], slots[-1] + 1
             betas[step] = small.tile([P, ROUNDS, CHUNKS], F32, name="beta", tag="beta")
             beta = betas[step]
+            nc.vector.reduce_sum(
+                out=beta[:, lo:hi, :],
+                in_=sums[step][:, 0 : ROUNDS * CHUNKS * 2].rearrange("p (r j c) -> p r j c", j=CHUNKS, c=2)[:, lo:hi],
+                axis=AX.X,
+            )
             nc.vector.tensor_tensor(
                 out=beta[:, lo:hi, :],
-                in0=sums[step][:, 0 : ROUNDS * CHUNKS, 0].rearrange("p (r j) -> p r j", j=CHUNKS)[:, lo:hi, :],
-                in1=scaling_tile(step)[:, 1, lo:hi].unsqueeze(2).to_broadcast([P, hi - lo, CHUNKS]),
+                in0=beta[:, lo:hi, :],
+                in1=alphas[step][:, 1, lo:hi].unsqueeze(2).to_broadcast([P, hi - lo, CHUNKS]),
                 op=ALU.add,
             )
             nc.vector.reciprocal(out=beta[:, lo:hi, :], in_=beta[:, lo:hi, :])
-            slots = slots_of(step, ROUNDS - 1)
-            if slots:
-                lo, hi = slots[0], slots[-1] + 1
+            hi = min(hi, ROUNDS - 1)
+            if lo < hi:
                 beta_sums[step] = small.tile([P, ROUNDS], F32, name="beta_sum", tag="beta_sum")
                 nc.vector.reduce_sum(out=beta_sums[step][:, lo:hi], in_=beta[:, lo:hi, :], axis=AX.X)
 
-        def row_sums(step, r):
-            if not is_image(step - r):
+        def dust_sums(step):
+            for r in range(ROUNDS - 1):
+                if is_image(row_image(step, r)):
+                    at = ROUNDS * CHUNKS * 2 + r
+                    nc.tensor.matmul(
+                        out=sums_tile(step)[:, at : at + 1],
+                        lhsT=mean_ones[:],
+                        rhs=beta_sums[step - 1][:, r : r + 1],
+                        start=True,
+                        stop=True,
+                    )
+
+        def spread_betas(step, r):
+            if not is_image(row_image(step, r)):
                 return
-            base = ROUNDS * CHUNKS
-            for j in range(CHUNKS):
-                nc.tensor.matmul(
-                    out=sums[step][:, base + r, :],
-                    lhsT=kern_t[step - r][:, j, :],
-                    rhs=betas[step][:, r, j : j + 1].to_broadcast([P, REPEAT]),
-                    start=(j == 0),
-                    stop=(j == CHUNKS - 1),
-                )
-            nc.tensor.matmul(
-                out=sums[step][:, base + ROUNDS + r, :],
-                lhsT=mean_ones[:],
-                rhs=beta_sums[step][:, r : r + 1].to_broadcast([P, REPEAT]),
-                start=True,
-                stop=True,
-            )
+            spread[r] = []
+            for half in range(HALVES):
+                bank = psum_t.tile([P, CHUNKS_PER_BANK, P], F32, name="spread", tag="flip")
+                for q in range(CHUNKS_PER_BANK):
+                    j = half * CHUNKS_PER_BANK + q
+                    nc.tensor.transpose(bank[:, q, :], betas[step - 1][:, r, j : j + 1].to_broadcast([P, P]), ident[:])
+                spread[r].append(bank)
+
+        def weigh_rows(step, r):
+            b = row_image(step, r)
+            if not is_image(b):
+                return
+            last = r == ROUNDS - 1
+            if last:
+                result = sk.tile([P, PIXELS], F32, name="result", tag="result")
+            for half in range(HALVES):
+                if last:
+                    nc.vector.scalar_tensor_tensor(
+                        out=result[:, half_cols(half)],
+                        in0=kern[b][:, half_cols(half)],
+                        scalar=alphas[step - 1][:, 0, r : r + 1],
+                        in1=spread[r][half][:].rearrange("p q n -> p (q n)"),
+                        op0=ALU.mult,
+                        op1=ALU.mult,
+                    )
+                else:
+                    unread = sk.tile([P, BANK], F32, name="unread", tag="unread", bufs=4)
+                    nc.vector.scalar_tensor_tensor(
+                        out=unread[:],
+                        in0=kern[b][:, half_cols(half)],
+                        scalar=1.0,
+                        in1=spread[r][half][:].rearrange("p q n -> p (q n)"),
+                        op0=ALU.mult,
+                        op1=ALU.mult,
+                        accum_out=row_acc_tile(step)[:, r + 1, half : half + 1],
+                    )
+            if last:
+                nc.sync.dma_start(out=out[b], in_=result[:])
 
         def new_alphas(step):
-            slots = slots_of(step, ROUNDS - 1)
-            if not slots:
+            lo, hi = slot_range(column_image, step + 1, ROUNDS)
+            if lo == hi:
                 return
-            lo, hi = slots[0], slots[-1] + 1
-            nc.vector.reciprocal(
-                out=scaling_tile(step + 1)[:, :, lo + 1 : hi + 1],
-                in_=sums[step][:, ROUNDS * CHUNKS :, 0].rearrange("p (k r) -> p k r", r=ROUNDS)[:, :, lo:hi],
-            )
+            alpha = alpha_tile(step + 1)
+            row_sum = small.tile([P, ROUNDS], F32, name="row_sum", tag="row_sum")
+            nc.vector.reduce_sum(out=row_sum[:, lo:hi], in_=row_accs[step][:, lo:hi, 0:HALVES], axis=AX.X)
+            nc.vector.reciprocal(out=alpha[:, 0, lo:hi], in_=row_sum[:, lo:hi])
+            if max(lo, 1) < hi:
+                at = ROUNDS * CHUNKS * 2
+                nc.vector.reciprocal(out=alpha[:, 1, max(lo, 1) : hi], in_=sums[step][:, at + max(lo, 1) - 1 : at + hi - 1])
+            alpha_parts[step + 1] = small.tile([P, ROUNDS, 2], BF16, name="alpha_part", tag="alpha_part")
+            parts = alpha_parts[step + 1]
+            nc.vector.tensor_copy(out=parts[:, lo:hi, 0], in_=alpha[:, 0, lo:hi])
+            nc.vector.tensor_tensor(out=parts[:, lo:hi, 1], in0=alpha[:, 0, lo:hi], in1=parts[:, lo:hi, 0], op=ALU.subtract)
 
-        def scale_columns(step):
-            b = step - (ROUNDS - 1)
-            if not is_image(b):
-                return
-            scaled_t[b] = sk.tile([P, CHUNKS, P], F32, name="scaled", tag="scaled", bufs=2)
-            nc.vector.tensor_tensor(
-                out=scaled_t[b][:],
-                in0=kern_t[b][:],
-                in1=betas[step][:, ROUNDS - 1, :].unsqueeze(2).to_broadcast([P, CHUNKS, P]),
-                op=ALU.mult,
-            )
-
-        def flip_back_and_store(step):
-            b = step - (ROUNDS - 1)
-            if not is_image(b):
-                return
-            result = sk.tile([P, PIXELS], F32, name="result", tag="result", bufs=2)
-            for half in range(HALVES):
-                back = psum_t.tile([P, CHUNKS_PER_BANK, P], F32, name="back", tag="flip")
-                for q in range(CHUNKS_PER_BANK):
-                    nc.tensor.transpose(back[:, q, :], scaled_t[b][:, half * CHUNKS_PER_BANK + q, :], ident[:])
-                nc.scalar.activation(
-                    out=result[:, half_cols(half)],
-                    in_=back[:].rearrange("p q n -> p (q n)"),
-                    func=ACT.Copy,
-                    scale=scaling_tile(step)[:, 0, ROUNDS - 1 : ROUNDS],
-                )
-            nc.scalar.dma_start(out=out[b], in_=result[:])
-
-        for s in range(IMAGES + 4 + ROUNDS - 1):
-            fresh, hidden, scored, step = s - 1, s - 2, s - 3, s - 4
+        for s in range(IMAGES + 6 + 2 * (ROUNDS - 1)):
+            grouped, hidden, scored, exped = s - 1, s - 2, s - 3, s - 4
             load_image(s)
-            if is_image(scored):
-                scaling_tile(scored)
+            if is_image(exped):
+                alpha_tile(s + 1)
             regroup_hidden(scored, 1)
-            regroup_image(fresh)
             hidden_pass(hidden, 0)
-            column_sums(step, 0)
+            regroup_image(grouped, 0)
+            spread_betas(s, 0)
+            quantise_image(hidden, 1)
+            weigh_rows(s, 0)
             hidden_pass(hidden, 1)
-            column_sums(step, 1)
+            spread_betas(s, 1)
             quantise_hidden(scored, 1)
+            weigh_rows(s, 1)
             hidden_pass(hidden, 2)
-            column_sums(step, 2)
-            new_betas(step)
+            regroup_image(grouped, 1)
+            spread_betas(s, 2)
+            low_parts(exped)
+            weigh_rows(s, 2)
             hidden_pass(hidden, 3)
-            cluster_scores(scored)
-            scale_columns(step)
-            row_tops(scored)
+            dust_sums(s)
+            column_sums(s, 0)
+            new_alphas(s)
+            quantise_image(grouped, 0)
             hidden_pass(hidden, 4)
-            row_sums(step, 0)
-            hidden_pass(hidden, 5)
-            row_sums(step, 1)
-            exponentials(scored)
+            regroup_image(grouped, 2)
+            column_sums(s, 1)
             regroup_hidden(hidden, 0)
-            hidden_pass(hidden, 6)
-            flip_back_and_store(step)
-            quantise_image(fresh)
+            hidden_pass(hidden, 5)
+            column_sums(s, 2)
+            new_betas(s)
             quantise_hidden(hidden, 0)
-            first_alpha(scored)
-            new_alphas(step)
+            hidden_pass(hidden, 6)
+            regroup_image(grouped, 3)
+            cluster_scores(scored)
+            row_tops(scored)
             hidden_pass(hidden, 7)
-            flip_kernel(scored)
+            exponentials(scored, s)

@@ -24,8 +24,11 @@ CHUNKS_PER_BANK = BANK // P
 ROUNDS = 3
 RUN = 4
 PIECES = 4
+SCALAR_PIECES = 3
 PIECE = PIXELS // PIECES
-BLOCK = 8
+PARTS = 2
+REPEAT = 4
+WIDTH = REPEAT * PARTS
 
 FLOPS = 2 * IMAGES * PIXELS * (CHANNELS * HIDDEN + HIDDEN * CLUSTERS)
 
@@ -46,7 +49,9 @@ def tile_salad_pa_t_kernel(tc, x, Ws1, bs1, Ws2, out):
     ):
         ident = consts.tile([P, P], F32)
         make_identity(nc, ident[:])
-        mean_ones = consts.tile([P, P], F32)
+        ident_bf = consts.tile([P, P], BF16)
+        make_identity(nc, ident_bf[:])
+        mean_ones = consts.tile([P, P], BF16)
         nc.vector.memset(mean_ones[:], 1.0 / PIXELS)
 
         w1_raw = consts.tile([P, PACK * CHANNELS], BF16)
@@ -87,8 +92,8 @@ def tile_salad_pa_t_kernel(tc, x, Ws1, bs1, Ws2, out):
         x_raw, x_grouped, x_codes, x_scales = {}, {}, {}, {}
         hs_planes, hs_grouped, hs_codes, hs_scales = {}, {}, {}, {}
         scores, neg_tops = {}, {}
-        kern, kern_lo = {}, {}
-        alphas, alpha_parts, row_accs, sums, betas, beta_sums, spread = {}, {}, {}, {}, {}, {}, {}
+        kern, kern_lo, kern_t, first_sums = {}, {}, {}, {}
+        alphas, alpha_parts, sums, betas, beta_parts = {}, {}, {}, {}, {}
 
         def is_image(b):
             return 0 <= b < IMAGES
@@ -115,7 +120,10 @@ def tile_salad_pa_t_kernel(tc, x, Ws1, bs1, Ws2, out):
                 x_grouped[b] = xs.tile([P, PIXELS, PACK], BF16, name="x_grouped", tag="x_grouped", align_bytes=64)
             cols = slice(piece * PIECE, (piece + 1) * PIECE)
             dst, src = regrouped(x_grouped[b][:, cols, :], x_raw[b][:, :, cols])
-            nc.scalar.copy(out=dst, in_=src)
+            if piece < SCALAR_PIECES:
+                nc.scalar.copy(out=dst, in_=src)
+            else:
+                nc.vector.tensor_copy(out=dst, in_=src)
 
         def quantise_image(b, half):
             if not is_image(b):
@@ -198,15 +206,11 @@ def tile_salad_pa_t_kernel(tc, x, Ws1, bs1, Ws2, out):
                 out=neg_tops[b][:], in0=top2[:, 0:1], scalar1=top2[:, 1:2], scalar2=-1.0, op0=ALU.max, op1=ALU.mult
             )
 
-        def row_acc_tile(step):
-            if step not in row_accs:
-                row_accs[step] = small.tile([P, ROUNDS, BLOCK], F32, name="row_acc", tag="row_acc")
-            return row_accs[step]
-
-        def exponentials(b, step):
+        def exponentials(b):
             if not is_image(b):
                 return
-            kern[b] = sk.tile([P, PIXELS], F32, name="kern", tag="kern", bufs=9)
+            kern[b] = sk.tile([P, PIXELS], F32, name="kern", tag="kern", bufs=6)
+            first_sums[b] = small.tile([P, HALVES], F32, name="first_sum", tag="first_sum")
             for half in range(HALVES):
                 nc.scalar.activation(
                     out=kern[b][:, half_cols(half)],
@@ -214,7 +218,7 @@ def tile_salad_pa_t_kernel(tc, x, Ws1, bs1, Ws2, out):
                     func=ACT.Exp,
                     bias=neg_tops[b][:, 0:1],
                     scale=1.0,
-                    accum_out=row_acc_tile(step + 1)[:, 0, half : half + 1],
+                    accum_out=first_sums[b][:, half : half + 1],
                 )
 
         def high_parts(b):
@@ -223,183 +227,192 @@ def tile_salad_pa_t_kernel(tc, x, Ws1, bs1, Ws2, out):
         def low_parts(b):
             if not is_image(b):
                 return
-            kern_lo[b] = sk.tile([P, PIXELS], BF16, name="kern_lo", tag="kern_lo", bufs=7)
+            kern_lo[b] = sk.tile([P, PIXELS], BF16, name="kern_lo", tag="kern_lo", bufs=5)
             nc.vector.tensor_tensor(out=kern_lo[b][:], in0=kern[b][:], in1=high_parts(b), op=ALU.subtract)
 
-        def column_image(step, r):
-            return step - 5 - 2 * r
+        def flip_kernel(b):
+            if not is_image(b):
+                return
+            kern_t[b] = sk.tile([P, PARTS, CHUNKS, P], BF16, name="kern_t", tag="kern_t", bufs=4)
+            flipped_hi = psum_t.tile([P, CHUNKS, P], BF16, name="flipped_hi", tag="flip")
+            for j in range(CHUNKS):
+                nc.tensor.matmul(
+                    out=flipped_hi[:, j, :],
+                    lhsT=high_parts(b)[:, j * P : (j + 1) * P],
+                    rhs=ident_bf[:],
+                    start=True,
+                    stop=True,
+                )
+            nc.scalar.copy(out=kern_t[b][:, 0], in_=flipped_hi[:])
+            flipped_lo = psum_t.tile([P, CHUNKS, P], BF16, name="flipped_lo", tag="flip")
+            for j in range(CHUNKS):
+                nc.tensor.transpose(flipped_lo[:, j, :], kern_lo[b][:, j * P : (j + 1) * P], ident_bf[:])
+            nc.scalar.copy(out=kern_t[b][:, 1], in_=flipped_lo[:])
 
-        def row_image(step, r):
-            return step - 6 - 2 * r
+        COLUMN_AT = 0
+        ROW_AT = COLUMN_AT + ROUNDS * CHUNKS * WIDTH
+        DUST_AT = ROW_AT + (ROUNDS - 1) * WIDTH
+        SUMS = DUST_AT + (ROUNDS - 1) * CHUNKS * PARTS
 
-        def slot_range(image_of, step, rounds):
-            slots = [r for r in range(rounds) if is_image(image_of(step, r))]
+        def image_in_round(step, r):
+            return step - 5 - r
+
+        def slot_range(step, rounds):
+            slots = [r for r in range(rounds) if is_image(image_in_round(step, r))]
             if not slots:
                 return 0, 0
             return slots[0], slots[-1] + 1
 
-        def alpha_tile(step):
-            if step not in alphas:
-                alphas[step] = small.tile([P, 2, ROUNDS], F32, name="alpha", tag="alpha")
-                nc.gpsimd.memset(alphas[step][:], 1.0)
-            return alphas[step]
+        def ones_tile(name):
+            fresh = small.tile([P, 2, ROUNDS], F32, name=name, tag=name)
+            nc.gpsimd.memset(fresh[:], 1.0)
+            return fresh
 
-        def sums_tile(step):
-            if step not in sums:
-                sums[step] = psum_v.tile([P, ROUNDS * CHUNKS * 2 + ROUNDS], F32, name="sums", tag="sums")
-            return sums[step]
+        def split(parts, values):
+            nc.vector.tensor_copy(out=parts[0], in_=values)
+            nc.vector.tensor_tensor(out=parts[1], in0=values, in1=parts[0], op=ALU.subtract)
+
+        def repeated(parts):
+            return parts.unsqueeze(1).to_broadcast([P, REPEAT, PARTS])
 
         def column_sums(step, r):
-            b = column_image(step, r)
+            b = image_in_round(step, r)
             if not is_image(b):
                 return
+            if step not in sums:
+                sums[step] = psum_v.tile([P, SUMS], F32, name="sums", tag="sums")
             for j in range(CHUNKS):
-                at = (r * CHUNKS + j) * 2
+                at = COLUMN_AT + (r * CHUNKS + j) * WIDTH
                 cols = slice(j * P, (j + 1) * P)
-                nc.tensor.matmul(
-                    out=sums_tile(step)[:, at : at + 2],
-                    lhsT=high_parts(b)[:, cols],
-                    rhs=alpha_parts[step][:, r, :],
-                    start=True,
-                    stop=False,
-                )
-                nc.tensor.matmul(
-                    out=sums_tile(step)[:, at : at + 2],
-                    lhsT=kern_lo[b][:, cols],
-                    rhs=alpha_parts[step][:, r, :],
-                    start=False,
-                    stop=True,
-                )
+                for part, rows in enumerate((high_parts(b), kern_lo[b][:])):
+                    nc.tensor.matmul(
+                        out=sums[step][:, at : at + WIDTH],
+                        lhsT=rows[:, cols],
+                        rhs=repeated(alpha_parts[step][:, r, :]),
+                        start=(part == 0),
+                        stop=(part == PARTS - 1),
+                    )
 
         def new_betas(step):
-            lo, hi = slot_range(column_image, step, ROUNDS)
+            lo, hi = slot_range(step, ROUNDS)
             if lo == hi:
                 return
             betas[step] = small.tile([P, ROUNDS, CHUNKS], F32, name="beta", tag="beta")
-            beta = betas[step]
+            beta = betas[step][:, lo:hi, :]
             nc.vector.reduce_sum(
-                out=beta[:, lo:hi, :],
-                in_=sums[step][:, 0 : ROUNDS * CHUNKS * 2].rearrange("p (r j c) -> p r j c", j=CHUNKS, c=2)[:, lo:hi],
+                out=beta,
+                in_=sums[step][:, COLUMN_AT:ROW_AT].rearrange("p (r j c) -> p r j c", j=CHUNKS, c=WIDTH)[:, lo:hi, :, 0:PARTS],
                 axis=AX.X,
             )
             nc.vector.tensor_tensor(
-                out=beta[:, lo:hi, :],
-                in0=beta[:, lo:hi, :],
+                out=beta,
+                in0=beta,
                 in1=alphas[step][:, 1, lo:hi].unsqueeze(2).to_broadcast([P, hi - lo, CHUNKS]),
                 op=ALU.add,
             )
-            nc.vector.reciprocal(out=beta[:, lo:hi, :], in_=beta[:, lo:hi, :])
-            hi = min(hi, ROUNDS - 1)
-            if lo < hi:
-                beta_sums[step] = small.tile([P, ROUNDS], F32, name="beta_sum", tag="beta_sum")
-                nc.vector.reduce_sum(out=beta_sums[step][:, lo:hi], in_=beta[:, lo:hi, :], axis=AX.X)
+            nc.vector.reciprocal(out=beta, in_=beta)
+            beta_parts[step] = small.tile([P, ROUNDS, CHUNKS, PARTS], BF16, name="beta_part", tag="beta_part")
+            split([beta_parts[step][:, lo:hi, :, part] for part in range(PARTS)], beta)
 
-        def dust_sums(step):
-            for r in range(ROUNDS - 1):
-                if is_image(row_image(step, r)):
-                    at = ROUNDS * CHUNKS * 2 + r
-                    nc.tensor.matmul(
-                        out=sums_tile(step)[:, at : at + 1],
-                        lhsT=mean_ones[:],
-                        rhs=beta_sums[step - 1][:, r : r + 1],
-                        start=True,
-                        stop=True,
-                    )
-
-        def spread_betas(step, r):
-            if not is_image(row_image(step, r)):
-                return
-            spread[r] = []
-            for half in range(HALVES):
-                bank = psum_t.tile([P, CHUNKS_PER_BANK, P], F32, name="spread", tag="flip")
-                for q in range(CHUNKS_PER_BANK):
-                    j = half * CHUNKS_PER_BANK + q
-                    nc.tensor.transpose(bank[:, q, :], betas[step - 1][:, r, j : j + 1].to_broadcast([P, P]), ident[:])
-                spread[r].append(bank)
-
-        def weigh_rows(step, r):
-            b = row_image(step, r)
+        def row_sums(step, r):
+            b = image_in_round(step, r)
             if not is_image(b):
                 return
-            last = r == ROUNDS - 1
-            if last:
-                result = sk.tile([P, PIXELS], F32, name="result", tag="result")
-            for half in range(HALVES):
-                if last:
-                    nc.vector.scalar_tensor_tensor(
-                        out=result[:, half_cols(half)],
-                        in0=kern[b][:, half_cols(half)],
-                        scalar=alphas[step - 1][:, 0, r : r + 1],
-                        in1=spread[r][half][:].rearrange("p q n -> p (q n)"),
-                        op0=ALU.mult,
-                        op1=ALU.mult,
+            at = ROW_AT + r * WIDTH
+            for j in range(CHUNKS):
+                for part in range(PARTS):
+                    nc.tensor.matmul(
+                        out=sums[step][:, at : at + WIDTH],
+                        lhsT=kern_t[b][:, part, j, :],
+                        rhs=repeated(beta_parts[step][:, r, j, :]),
+                        start=(j == 0 and part == 0),
+                        stop=(j == CHUNKS - 1 and part == PARTS - 1),
                     )
-                else:
-                    unread = sk.tile([P, BANK], F32, name="unread", tag="unread", bufs=4)
-                    nc.vector.scalar_tensor_tensor(
-                        out=unread[:],
-                        in0=kern[b][:, half_cols(half)],
-                        scalar=1.0,
-                        in1=spread[r][half][:].rearrange("p q n -> p (q n)"),
-                        op0=ALU.mult,
-                        op1=ALU.mult,
-                        accum_out=row_acc_tile(step)[:, r + 1, half : half + 1],
-                    )
-            if last:
-                nc.sync.dma_start(out=out[b], in_=result[:])
+            at = DUST_AT + r * CHUNKS * PARTS
+            nc.tensor.matmul(
+                out=sums[step][:, at : at + CHUNKS * PARTS],
+                lhsT=mean_ones[:],
+                rhs=beta_parts[step][:, r].rearrange("p j c -> p (j c)"),
+                start=True,
+                stop=True,
+            )
 
         def new_alphas(step):
-            lo, hi = slot_range(column_image, step + 1, ROUNDS)
+            lo, hi = slot_range(step + 1, ROUNDS)
             if lo == hi:
                 return
-            alpha = alpha_tile(step + 1)
-            row_sum = small.tile([P, ROUNDS], F32, name="row_sum", tag="row_sum")
-            nc.vector.reduce_sum(out=row_sum[:, lo:hi], in_=row_accs[step][:, lo:hi, 0:HALVES], axis=AX.X)
-            nc.vector.reciprocal(out=alpha[:, 0, lo:hi], in_=row_sum[:, lo:hi])
-            if max(lo, 1) < hi:
-                at = ROUNDS * CHUNKS * 2
-                nc.vector.reciprocal(out=alpha[:, 1, max(lo, 1) : hi], in_=sums[step][:, at + max(lo, 1) - 1 : at + hi - 1])
-            alpha_parts[step + 1] = small.tile([P, ROUNDS, 2], BF16, name="alpha_part", tag="alpha_part")
-            parts = alpha_parts[step + 1]
-            nc.vector.tensor_copy(out=parts[:, lo:hi, 0], in_=alpha[:, 0, lo:hi])
-            nc.vector.tensor_tensor(out=parts[:, lo:hi, 1], in0=alpha[:, 0, lo:hi], in1=parts[:, lo:hi, 0], op=ALU.subtract)
+            below = ones_tile("below")
+            if lo == 0:
+                nc.vector.reduce_sum(out=below[:, 0, 0:1], in_=first_sums[image_in_round(step + 1, 0)][:], axis=AX.X)
+            old = max(lo, 1)
+            if old < hi:
+                nc.vector.reduce_sum(
+                    out=below[:, 0, old:hi],
+                    in_=sums[step][:, ROW_AT:DUST_AT].rearrange("p (r c) -> p r c", c=WIDTH)[:, old - 1 : hi - 1, 0:PARTS],
+                    axis=AX.X,
+                )
+                nc.vector.reduce_sum(
+                    out=below[:, 1, old:hi],
+                    in_=sums[step][:, DUST_AT:SUMS].rearrange("p (r c) -> p r c", c=CHUNKS * PARTS)[:, old - 1 : hi - 1],
+                    axis=AX.X,
+                )
+            alphas[step + 1] = small.tile([P, 2, ROUNDS], F32, name="alpha", tag="alpha")
+            nc.vector.reciprocal(out=alphas[step + 1][:, :, lo:hi], in_=below[:, :, lo:hi])
+            alpha_parts[step + 1] = small.tile([P, ROUNDS, PARTS], BF16, name="alpha_part", tag="alpha_part")
+            split([alpha_parts[step + 1][:, lo:hi, part] for part in range(PARTS)], alphas[step + 1][:, 0, lo:hi])
 
-        for s in range(IMAGES + 6 + 2 * (ROUNDS - 1)):
+        def scale_and_store(step):
+            r = ROUNDS - 1
+            b = image_in_round(step, r)
+            if not is_image(b):
+                return
+            result = sk.tile([P, PIXELS], F32, name="result", tag="result")
+            for half in range(HALVES):
+                spread = psum_t.tile([P, CHUNKS_PER_BANK, P], F32, name="spread", tag="flip")
+                for q in range(CHUNKS_PER_BANK):
+                    j = half * CHUNKS_PER_BANK + q
+                    nc.tensor.transpose(spread[:, q, :], betas[step][:, r, j : j + 1].to_broadcast([P, P]), ident[:])
+                nc.vector.scalar_tensor_tensor(
+                    out=result[:, half_cols(half)],
+                    in0=kern[b][:, half_cols(half)],
+                    scalar=alphas[step][:, 0, r : r + 1],
+                    in1=spread[:].rearrange("p q n -> p (q n)"),
+                    op0=ALU.mult,
+                    op1=ALU.mult,
+                )
+            nc.sync.dma_start(out=out[b], in_=result[:])
+
+        for s in range(IMAGES + 5 + ROUNDS - 1):
             grouped, hidden, scored, exped = s - 1, s - 2, s - 3, s - 4
             load_image(s)
-            if is_image(exped):
-                alpha_tile(s + 1)
             regroup_hidden(scored, 1)
             hidden_pass(hidden, 0)
             regroup_image(grouped, 0)
-            spread_betas(s, 0)
+            column_sums(s, 0)
             quantise_image(hidden, 1)
-            weigh_rows(s, 0)
             hidden_pass(hidden, 1)
-            spread_betas(s, 1)
-            quantise_hidden(scored, 1)
-            weigh_rows(s, 1)
+            column_sums(s, 1)
+            low_parts(exped)
             hidden_pass(hidden, 2)
             regroup_image(grouped, 1)
-            spread_betas(s, 2)
-            low_parts(exped)
-            weigh_rows(s, 2)
-            hidden_pass(hidden, 3)
-            dust_sums(s)
-            column_sums(s, 0)
-            new_alphas(s)
-            quantise_image(grouped, 0)
-            hidden_pass(hidden, 4)
-            regroup_image(grouped, 2)
-            column_sums(s, 1)
-            regroup_hidden(hidden, 0)
-            hidden_pass(hidden, 5)
             column_sums(s, 2)
-            new_betas(s)
-            quantise_hidden(hidden, 0)
-            hidden_pass(hidden, 6)
+            quantise_hidden(scored, 1)
             regroup_image(grouped, 3)
+            new_betas(s)
+            hidden_pass(hidden, 3)
             cluster_scores(scored)
             row_tops(scored)
+            hidden_pass(hidden, 4)
+            flip_kernel(exped)
+            hidden_pass(hidden, 5)
+            regroup_image(grouped, 2)
+            row_sums(s, 0)
+            quantise_image(grouped, 0)
+            hidden_pass(hidden, 6)
+            row_sums(s, 1)
+            scale_and_store(s)
+            regroup_hidden(hidden, 0)
+            new_alphas(s)
+            quantise_hidden(hidden, 0)
             hidden_pass(hidden, 7)
-            exponentials(scored, s)
+            exponentials(scored)

@@ -24,7 +24,7 @@ CHUNKS_PER_BANK = BANK // P
 ROUNDS = 3
 RUN = 4
 PIECES = 4
-SCALAR_PIECES = 3
+SCALAR_PIECES = 2
 PIECE = PIXELS // PIECES
 PARTS = 2
 REPEAT = 4
@@ -91,9 +91,9 @@ def tile_salad_pa_t_kernel(tc, x, Ws1, bs1, Ws2, out):
 
         x_raw, x_grouped, x_codes, x_scales = {}, {}, {}, {}
         hs_planes, hs_grouped, hs_codes, hs_scales = {}, {}, {}, {}
-        scores, neg_tops = {}, {}
+        scores, tops, neg_tops = {}, {}, {}
         kern, kern_lo, kern_t, first_sums = {}, {}, {}, {}
-        alphas, alpha_parts, sums, betas, beta_parts = {}, {}, {}, {}, {}
+        alphas, alpha_parts, belows, sums, betas, beta_parts, spreads, results = {}, {}, {}, {}, {}, {}, {}, {}
 
         def is_image(b):
             return 0 <= b < IMAGES
@@ -195,15 +195,24 @@ def tile_salad_pa_t_kernel(tc, x, Ws1, bs1, Ws2, out):
                 )
                 scores[b].append(score)
 
-        def row_tops(b):
+        def half_tops(b, half):
             if not is_image(b):
                 return
-            top2 = small.tile([P, HALVES], F32, name="top2", tag="top2")
-            for half in range(HALVES):
-                nc.vector.reduce_max(out=top2[:, half : half + 1], in_=scores[b][half][:], axis=AX.X)
+            if half == 0:
+                tops[b] = small.tile([P, HALVES], F32, name="top", tag="top")
+            nc.vector.reduce_max(out=tops[b][:, half : half + 1], in_=scores[b][half][:], axis=AX.X)
+
+        def negated_tops(b):
+            if not is_image(b):
+                return
             neg_tops[b] = small.tile([P, 1], F32, name="neg_top", tag="neg_top")
             nc.vector.tensor_scalar(
-                out=neg_tops[b][:], in0=top2[:, 0:1], scalar1=top2[:, 1:2], scalar2=-1.0, op0=ALU.max, op1=ALU.mult
+                out=neg_tops[b][:],
+                in0=tops[b][:, 0:1],
+                scalar1=tops[b][:, 1:2],
+                scalar2=-1.0,
+                op0=ALU.max,
+                op1=ALU.mult,
             )
 
         def exponentials(b):
@@ -268,9 +277,11 @@ def tile_salad_pa_t_kernel(tc, x, Ws1, bs1, Ws2, out):
             nc.gpsimd.memset(fresh[:], 1.0)
             return fresh
 
-        def split(parts, values):
-            nc.vector.tensor_copy(out=parts[0], in_=values)
-            nc.vector.tensor_tensor(out=parts[1], in0=values, in1=parts[0], op=ALU.subtract)
+        def split(high, low, values, part):
+            if part == 0:
+                nc.vector.tensor_copy(out=high, in_=values)
+            else:
+                nc.vector.tensor_tensor(out=low, in0=values, in1=high, op=ALU.subtract)
 
         def repeated(parts):
             return parts.unsqueeze(1).to_broadcast([P, REPEAT, PARTS])
@@ -293,26 +304,44 @@ def tile_salad_pa_t_kernel(tc, x, Ws1, bs1, Ws2, out):
                         stop=(part == PARTS - 1),
                     )
 
-        def new_betas(step):
+        def sum_columns(step):
             lo, hi = slot_range(step, ROUNDS)
             if lo == hi:
                 return
             betas[step] = small.tile([P, ROUNDS, CHUNKS], F32, name="beta", tag="beta")
-            beta = betas[step][:, lo:hi, :]
             nc.vector.reduce_sum(
-                out=beta,
-                in_=sums[step][:, COLUMN_AT:ROW_AT].rearrange("p (r j c) -> p r j c", j=CHUNKS, c=WIDTH)[:, lo:hi, :, 0:PARTS],
+                out=betas[step][:, lo:hi, :],
+                in_=sums[step][:, COLUMN_AT:ROW_AT].rearrange("p (r j c) -> p r j c", j=CHUNKS, c=WIDTH)[
+                    :, lo:hi, :, 0:PARTS
+                ],
                 axis=AX.X,
             )
+
+        def add_dustbin(step):
+            lo, hi = slot_range(step, ROUNDS)
+            if lo == hi:
+                return
             nc.vector.tensor_tensor(
-                out=beta,
-                in0=beta,
+                out=betas[step][:, lo:hi, :],
+                in0=betas[step][:, lo:hi, :],
                 in1=alphas[step][:, 1, lo:hi].unsqueeze(2).to_broadcast([P, hi - lo, CHUNKS]),
                 op=ALU.add,
             )
-            nc.vector.reciprocal(out=beta, in_=beta)
-            beta_parts[step] = small.tile([P, ROUNDS, CHUNKS, PARTS], BF16, name="beta_part", tag="beta_part")
-            split([beta_parts[step][:, lo:hi, :, part] for part in range(PARTS)], beta)
+
+        def invert_columns(step):
+            lo, hi = slot_range(step, ROUNDS)
+            if lo == hi:
+                return
+            nc.vector.reciprocal(out=betas[step][:, lo:hi, :], in_=betas[step][:, lo:hi, :])
+
+        def split_betas(step, part):
+            lo, hi = slot_range(step, ROUNDS)
+            if lo == hi:
+                return
+            if part == 0:
+                beta_parts[step] = small.tile([P, ROUNDS, CHUNKS, PARTS], BF16, name="beta_part", tag="beta_part")
+            parts = beta_parts[step][:, lo:hi]
+            split(parts[:, :, :, 0], parts[:, :, :, 1], betas[step][:, lo:hi, :], part)
 
         def row_sums(step, r):
             b = image_in_round(step, r)
@@ -337,11 +366,16 @@ def tile_salad_pa_t_kernel(tc, x, Ws1, bs1, Ws2, out):
                 stop=True,
             )
 
-        def new_alphas(step):
+        def prepare_sums(step):
+            lo, hi = slot_range(step + 1, ROUNDS)
+            if lo < hi:
+                belows[step] = ones_tile("below")
+
+        def sum_rows(step):
             lo, hi = slot_range(step + 1, ROUNDS)
             if lo == hi:
                 return
-            below = ones_tile("below")
+            below = belows[step]
             if lo == 0:
                 nc.vector.reduce_sum(out=below[:, 0, 0:1], in_=first_sums[image_in_round(step + 1, 0)][:], axis=AX.X)
             old = max(lo, 1)
@@ -356,35 +390,54 @@ def tile_salad_pa_t_kernel(tc, x, Ws1, bs1, Ws2, out):
                     in_=sums[step][:, DUST_AT:SUMS].rearrange("p (r c) -> p r c", c=CHUNKS * PARTS)[:, old - 1 : hi - 1],
                     axis=AX.X,
                 )
-            alphas[step + 1] = small.tile([P, 2, ROUNDS], F32, name="alpha", tag="alpha")
-            nc.vector.reciprocal(out=alphas[step + 1][:, :, lo:hi], in_=below[:, :, lo:hi])
-            alpha_parts[step + 1] = small.tile([P, ROUNDS, PARTS], BF16, name="alpha_part", tag="alpha_part")
-            split([alpha_parts[step + 1][:, lo:hi, part] for part in range(PARTS)], alphas[step + 1][:, 0, lo:hi])
 
-        def scale_and_store(step):
+        def invert_rows(step):
+            lo, hi = slot_range(step + 1, ROUNDS)
+            if lo == hi:
+                return
+            alphas[step + 1] = small.tile([P, 2, ROUNDS], F32, name="alpha", tag="alpha")
+            nc.vector.reciprocal(out=alphas[step + 1][:, :, lo:hi], in_=belows[step][:, :, lo:hi])
+
+        def split_alphas(step, part):
+            lo, hi = slot_range(step + 1, ROUNDS)
+            if lo == hi:
+                return
+            if part == 0:
+                alpha_parts[step + 1] = small.tile([P, ROUNDS, PARTS], BF16, name="alpha_part", tag="alpha_part")
+            parts = alpha_parts[step + 1][:, lo:hi]
+            split(parts[:, :, 0], parts[:, :, 1], alphas[step + 1][:, 0, lo:hi], part)
+
+        def spread_betas(step, half):
+            r = ROUNDS - 1
+            if not is_image(image_in_round(step, r)):
+                return
+            spreads[half] = psum_t.tile([P, CHUNKS_PER_BANK, P], F32, name="spread", tag="flip")
+            for q in range(CHUNKS_PER_BANK):
+                j = half * CHUNKS_PER_BANK + q
+                nc.tensor.transpose(spreads[half][:, q, :], betas[step][:, r, j : j + 1].to_broadcast([P, P]), ident[:])
+
+        def scale_and_store(step, half):
             r = ROUNDS - 1
             b = image_in_round(step, r)
             if not is_image(b):
                 return
-            result = sk.tile([P, PIXELS], F32, name="result", tag="result")
-            for half in range(HALVES):
-                spread = psum_t.tile([P, CHUNKS_PER_BANK, P], F32, name="spread", tag="flip")
-                for q in range(CHUNKS_PER_BANK):
-                    j = half * CHUNKS_PER_BANK + q
-                    nc.tensor.transpose(spread[:, q, :], betas[step][:, r, j : j + 1].to_broadcast([P, P]), ident[:])
-                nc.vector.scalar_tensor_tensor(
-                    out=result[:, half_cols(half)],
-                    in0=kern[b][:, half_cols(half)],
-                    scalar=alphas[step][:, 0, r : r + 1],
-                    in1=spread[:].rearrange("p q n -> p (q n)"),
-                    op0=ALU.mult,
-                    op1=ALU.mult,
-                )
-            nc.sync.dma_start(out=out[b], in_=result[:])
+            if half == 0:
+                results[b] = sk.tile([P, PIXELS], F32, name="result", tag="result")
+            nc.vector.scalar_tensor_tensor(
+                out=results[b][:, half_cols(half)],
+                in0=kern[b][:, half_cols(half)],
+                scalar=alphas[step][:, 0, r : r + 1],
+                in1=spreads[half][:].rearrange("p q n -> p (q n)"),
+                op0=ALU.mult,
+                op1=ALU.mult,
+            )
+            if half == HALVES - 1:
+                nc.sync.dma_start(out=out[b], in_=results[b][:])
 
         for s in range(IMAGES + 5 + ROUNDS - 1):
             grouped, hidden, scored, exped = s - 1, s - 2, s - 3, s - 4
             load_image(s)
+            prepare_sums(s)
             regroup_hidden(scored, 1)
             hidden_pass(hidden, 0)
             regroup_image(grouped, 0)
@@ -392,27 +445,39 @@ def tile_salad_pa_t_kernel(tc, x, Ws1, bs1, Ws2, out):
             quantise_image(hidden, 1)
             hidden_pass(hidden, 1)
             column_sums(s, 1)
-            low_parts(exped)
             hidden_pass(hidden, 2)
             regroup_image(grouped, 1)
             column_sums(s, 2)
+            sum_columns(s)
+            low_parts(exped)
+            add_dustbin(s)
             quantise_hidden(scored, 1)
-            regroup_image(grouped, 3)
-            new_betas(s)
+            invert_columns(s)
             hidden_pass(hidden, 3)
             cluster_scores(scored)
-            row_tops(scored)
+            regroup_image(grouped, 2)
+            split_betas(s, 0)
             hidden_pass(hidden, 4)
             flip_kernel(exped)
+            half_tops(scored, 0)
+            split_betas(s, 1)
+            half_tops(scored, 1)
+            spread_betas(s, 0)
             hidden_pass(hidden, 5)
-            regroup_image(grouped, 2)
             row_sums(s, 0)
-            quantise_image(grouped, 0)
+            regroup_image(grouped, 3)
+            negated_tops(scored)
             hidden_pass(hidden, 6)
             row_sums(s, 1)
-            scale_and_store(s)
+            spread_betas(s, 1)
+            quantise_image(grouped, 0)
+            sum_rows(s)
+            scale_and_store(s, 0)
+            invert_rows(s)
+            scale_and_store(s, 1)
+            split_alphas(s, 0)
             regroup_hidden(hidden, 0)
-            new_alphas(s)
+            split_alphas(s, 1)
             quantise_hidden(hidden, 0)
             hidden_pass(hidden, 7)
             exponentials(scored)

@@ -45,7 +45,6 @@ def tile_salad_pa_t_kernel(tc, x, Ws1, bs1, Ws2, out):
         tc.psum_pool(name="psum_p", bufs=2) as psum_p,
         tc.psum_pool(name="psum_t", bufs=3) as psum_t,
         tc.psum_pool(name="psum_v", bufs=1) as psum_v,
-        tc.manual_schedule(),
     ):
         ident = consts.tile([P, P], F32)
         make_identity(nc, ident[:])

@@ -26,8 +26,16 @@ RUN = 4
 PIECES = 4
 SCALAR_PIECES = 2
 PIECE = PIXELS // PIECES
+PAIR = 2
+PAIRS = IMAGES // PAIR
+LEAD = 3
+SLOTS = ROUNDS * PAIR
+OLD = PAIR
+ROWS = SLOTS - PAIR
 PARTS = 2
 REPEAT = 4
+KINDS = 2
+SLOT = 8
 WIDTH = REPEAT * PARTS
 
 FLOPS = 2 * IMAGES * PIXELS * (CHANNELS * HIDDEN + HIDDEN * CLUSTERS)
@@ -50,8 +58,10 @@ def tile_salad_pa_t_kernel(tc, x, Ws1, bs1, Ws2, out):
         make_identity(nc, ident[:])
         ident_bf = consts.tile([P, P], BF16)
         make_identity(nc, ident_bf[:])
-        mean_ones = consts.tile([P, P], BF16)
-        nc.vector.memset(mean_ones[:], 1.0 / PIXELS)
+        pixel_mean = consts.tile([P, P], BF16)
+        nc.vector.memset(pixel_mean[:], 1.0 / PIXELS)
+        row_mean = consts.tile([P, P], BF16)
+        nc.vector.memset(row_mean[:], 1.0 / P)
 
         w1_raw = consts.tile([P, PACK * CHANNELS], BF16)
         nc.sync.dma_start(out=w1_raw[:], in_=Ws1.rearrange("(p t) c -> p (t c)", t=PACK))
@@ -217,7 +227,7 @@ def tile_salad_pa_t_kernel(tc, x, Ws1, bs1, Ws2, out):
         def exponentials(b):
             if not is_image(b):
                 return
-            kern[b] = sk.tile([P, PIXELS], F32, name="kern", tag="kern", bufs=6)
+            kern[b] = sk.tile([P, PIXELS], F32, name="kern", tag="kern", bufs=10)
             first_sums[b] = small.tile([P, HALVES], F32, name="first_sum", tag="first_sum")
             for half in range(HALVES):
                 nc.scalar.activation(
@@ -235,13 +245,13 @@ def tile_salad_pa_t_kernel(tc, x, Ws1, bs1, Ws2, out):
         def low_parts(b):
             if not is_image(b):
                 return
-            kern_lo[b] = sk.tile([P, PIXELS], BF16, name="kern_lo", tag="kern_lo", bufs=5)
+            kern_lo[b] = sk.tile([P, PIXELS], BF16, name="kern_lo", tag="kern_lo", bufs=8)
             nc.vector.tensor_tensor(out=kern_lo[b][:], in0=kern[b][:], in1=high_parts(b), op=ALU.subtract)
 
         def flip_kernel(b):
             if not is_image(b):
                 return
-            kern_t[b] = sk.tile([P, PARTS, CHUNKS, P], BF16, name="kern_t", tag="kern_t", bufs=4)
+            kern_t[b] = sk.tile([P, PARTS, CHUNKS, P], BF16, name="kern_t", tag="kern_t", bufs=7)
             flipped_hi = psum_t.tile([P, CHUNKS, P], BF16, name="flipped_hi", tag="flip")
             for j in range(CHUNKS):
                 nc.tensor.matmul(
@@ -258,23 +268,17 @@ def tile_salad_pa_t_kernel(tc, x, Ws1, bs1, Ws2, out):
             nc.scalar.copy(out=kern_t[b][:, 1], in_=flipped_lo[:])
 
         COLUMN_AT = 0
-        ROW_AT = COLUMN_AT + ROUNDS * CHUNKS * WIDTH
-        DUST_AT = ROW_AT + (ROUNDS - 1) * WIDTH
-        SUMS = DUST_AT + (ROUNDS - 1) * CHUNKS * PARTS
+        ROW_AT = COLUMN_AT + SLOTS * CHUNKS * WIDTH
+        SUMS = ROW_AT + ROWS * KINDS * WIDTH
 
-        def image_in_round(step, r):
-            return step - 5 - r
+        def image_in_slot(turn, slot):
+            r, e = divmod(slot, PAIR)
+            pair = turn - LEAD - r
+            return pair * PAIR + e if 0 <= pair < PAIRS else -1
 
-        def slot_range(step, rounds):
-            slots = [r for r in range(rounds) if is_image(image_in_round(step, r))]
-            if not slots:
-                return 0, 0
-            return slots[0], slots[-1] + 1
-
-        def ones_tile(name):
-            fresh = small.tile([P, 2, ROUNDS], F32, name=name, tag=name)
-            nc.gpsimd.memset(fresh[:], 1.0)
-            return fresh
+        def slot_range(turn, slots):
+            held = [slot for slot in range(slots) if is_image(image_in_slot(turn, slot))]
+            return (held[0], held[-1] + 1) if held else (0, 0)
 
         def split(high, low, values, part):
             if part == 0:
@@ -282,150 +286,152 @@ def tile_salad_pa_t_kernel(tc, x, Ws1, bs1, Ws2, out):
             else:
                 nc.vector.tensor_tensor(out=low, in0=values, in1=high, op=ALU.subtract)
 
-        def repeated(parts):
-            return parts.unsqueeze(1).to_broadcast([P, REPEAT, PARTS])
+        def repeated(parts, times=REPEAT):
+            return parts.unsqueeze(1).to_broadcast([P, times, PARTS])
 
-        def column_sums(step, r):
-            b = image_in_round(step, r)
+        def column_sums(turn, slot):
+            b = image_in_slot(turn, slot)
             if not is_image(b):
                 return
-            if step not in sums:
-                sums[step] = psum_v.tile([P, SUMS], F32, name="sums", tag="sums")
+            if turn not in sums:
+                sums[turn] = psum_v.tile([P, SUMS], F32, name="sums", tag="sums")
+            at = COLUMN_AT + slot * CHUNKS * WIDTH
+            nc.tensor.matmul(
+                out=sums[turn][:, at : at + CHUNKS * WIDTH],
+                lhsT=row_mean[:],
+                rhs=repeated(alpha_parts[turn][:, slot, 1, :], CHUNKS * REPEAT),
+                start=True,
+                stop=False,
+            )
             for j in range(CHUNKS):
-                at = COLUMN_AT + (r * CHUNKS + j) * WIDTH
                 cols = slice(j * P, (j + 1) * P)
                 for part, rows in enumerate((high_parts(b), kern_lo[b][:])):
                     nc.tensor.matmul(
-                        out=sums[step][:, at : at + WIDTH],
+                        out=sums[turn][:, at + j * WIDTH : at + (j + 1) * WIDTH],
                         lhsT=rows[:, cols],
-                        rhs=repeated(alpha_parts[step][:, r, :]),
-                        start=(part == 0),
-                        stop=(part == PARTS - 1),
+                        rhs=repeated(alpha_parts[turn][:, slot, 0, :]),
+                        start=False,
+                        stop=(j == CHUNKS - 1 and part == PARTS - 1),
                     )
 
-        def sum_columns(step):
-            lo, hi = slot_range(step, ROUNDS)
+        def sum_columns(turn):
+            lo, hi = slot_range(turn, SLOTS)
             if lo == hi:
                 return
-            betas[step] = small.tile([P, ROUNDS, CHUNKS], F32, name="beta", tag="beta")
+            betas[turn] = small.tile([P, SLOTS, CHUNKS], F32, name="beta", tag="beta")
             nc.vector.reduce_sum(
-                out=betas[step][:, lo:hi, :],
-                in_=sums[step][:, COLUMN_AT:ROW_AT].rearrange("p (r j c) -> p r j c", j=CHUNKS, c=WIDTH)[
+                out=betas[turn][:, lo:hi, :],
+                in_=sums[turn][:, COLUMN_AT:ROW_AT].rearrange("p (r j c) -> p r j c", j=CHUNKS, c=WIDTH)[
                     :, lo:hi, :, 0:PARTS
                 ],
                 axis=AX.X,
             )
 
-        def add_dustbin(step):
-            lo, hi = slot_range(step, ROUNDS)
+        def invert_columns(turn):
+            lo, hi = slot_range(turn, SLOTS)
             if lo == hi:
                 return
-            nc.vector.tensor_tensor(
-                out=betas[step][:, lo:hi, :],
-                in0=betas[step][:, lo:hi, :],
-                in1=alphas[step][:, 1, lo:hi].unsqueeze(2).to_broadcast([P, hi - lo, CHUNKS]),
-                op=ALU.add,
-            )
+            nc.vector.reciprocal(out=betas[turn][:, lo:hi, :], in_=betas[turn][:, lo:hi, :])
 
-        def invert_columns(step):
-            lo, hi = slot_range(step, ROUNDS)
-            if lo == hi:
-                return
-            nc.vector.reciprocal(out=betas[step][:, lo:hi, :], in_=betas[step][:, lo:hi, :])
-
-        def split_betas(step, part):
-            lo, hi = slot_range(step, ROUNDS)
+        def split_betas(turn, part):
+            lo, hi = slot_range(turn, ROWS)
             if lo == hi:
                 return
             if part == 0:
-                beta_parts[step] = small.tile([P, ROUNDS, CHUNKS, PARTS], BF16, name="beta_part", tag="beta_part")
-            parts = beta_parts[step][:, lo:hi]
-            split(parts[:, :, :, 0], parts[:, :, :, 1], betas[step][:, lo:hi, :], part)
+                beta_parts[turn] = small.tile([P, ROWS, CHUNKS, PARTS], BF16, name="beta_part", tag="beta_part")
+            parts = beta_parts[turn][:, lo:hi]
+            split(parts[:, :, :, 0], parts[:, :, :, 1], betas[turn][:, lo:hi, :], part)
 
-        def row_sums(step, r):
-            b = image_in_round(step, r)
+        def row_sums(turn, slot):
+            b = image_in_slot(turn, slot)
             if not is_image(b):
                 return
-            at = ROW_AT + r * WIDTH
+            at = ROW_AT + slot * KINDS * WIDTH
             for j in range(CHUNKS):
                 for part in range(PARTS):
                     nc.tensor.matmul(
-                        out=sums[step][:, at : at + WIDTH],
+                        out=sums[turn][:, at : at + WIDTH],
                         lhsT=kern_t[b][:, part, j, :],
-                        rhs=repeated(beta_parts[step][:, r, j, :]),
+                        rhs=repeated(beta_parts[turn][:, slot, j, :]),
                         start=(j == 0 and part == 0),
                         stop=(j == CHUNKS - 1 and part == PARTS - 1),
                     )
-            at = DUST_AT + r * CHUNKS * PARTS
-            nc.tensor.matmul(
-                out=sums[step][:, at : at + CHUNKS * PARTS],
-                lhsT=mean_ones[:],
-                rhs=beta_parts[step][:, r].rearrange("p j c -> p (j c)"),
-                start=True,
-                stop=True,
+            at = at + WIDTH
+            for j in range(CHUNKS):
+                nc.tensor.matmul(
+                    out=sums[turn][:, at : at + WIDTH],
+                    lhsT=pixel_mean[:],
+                    rhs=repeated(beta_parts[turn][:, slot, j, :]),
+                    start=(j == 0),
+                    stop=(j == CHUNKS - 1),
+                )
+
+        def prepare_sums(turn):
+            lo, hi = slot_range(turn + 1, SLOTS)
+            if lo == hi:
+                return
+            belows[turn] = small.tile([P, SLOTS, SLOT], F32, name="below", tag="below")
+            nc.gpsimd.memset(belows[turn][:], 1.0)
+            for slot in range(lo, min(hi, OLD)):
+                halves = first_sums[image_in_slot(turn + 1, slot)]
+                nc.gpsimd.tensor_tensor(
+                    out=belows[turn][:, slot, 0:1], in0=halves[:, 0:1], in1=halves[:, 1:2], op=ALU.add
+                )
+
+        def sum_rows(turn):
+            lo, hi = slot_range(turn + 1, SLOTS)
+            old = max(lo, OLD)
+            if old >= hi:
+                return
+            nc.vector.reduce_sum(
+                out=belows[turn][:, old:hi, 0:KINDS],
+                in_=sums[turn][:, ROW_AT:SUMS].rearrange("p (r k c) -> p r k c", k=KINDS, c=WIDTH)[
+                    :, old - OLD : hi - OLD, :, 0:PARTS
+                ],
+                axis=AX.X,
             )
 
-        def prepare_sums(step):
-            lo, hi = slot_range(step + 1, ROUNDS)
-            if lo < hi:
-                belows[step] = ones_tile("below")
-
-        def sum_rows(step):
-            lo, hi = slot_range(step + 1, ROUNDS)
+        def invert_rows(turn):
+            lo, hi = slot_range(turn + 1, SLOTS)
             if lo == hi:
                 return
-            below = belows[step]
-            if lo == 0:
-                nc.vector.reduce_sum(out=below[:, 0, 0:1], in_=first_sums[image_in_round(step + 1, 0)][:], axis=AX.X)
-            old = max(lo, 1)
-            if old < hi:
-                nc.vector.reduce_sum(
-                    out=below[:, 0, old:hi],
-                    in_=sums[step][:, ROW_AT:DUST_AT].rearrange("p (r c) -> p r c", c=WIDTH)[:, old - 1 : hi - 1, 0:PARTS],
-                    axis=AX.X,
-                )
-                nc.vector.reduce_sum(
-                    out=below[:, 1, old:hi],
-                    in_=sums[step][:, DUST_AT:SUMS].rearrange("p (r c) -> p r c", c=CHUNKS * PARTS)[:, old - 1 : hi - 1],
-                    axis=AX.X,
-                )
+            alphas[turn + 1] = small.tile([P, SLOTS, KINDS], F32, name="alpha", tag="alpha")
+            nc.vector.reciprocal(out=alphas[turn + 1][:, lo:hi, :], in_=belows[turn][:, lo:hi, 0:KINDS])
 
-        def invert_rows(step):
-            lo, hi = slot_range(step + 1, ROUNDS)
-            if lo == hi:
-                return
-            alphas[step + 1] = small.tile([P, 2, ROUNDS], F32, name="alpha", tag="alpha")
-            nc.vector.reciprocal(out=alphas[step + 1][:, :, lo:hi], in_=belows[step][:, :, lo:hi])
-
-        def split_alphas(step, part):
-            lo, hi = slot_range(step + 1, ROUNDS)
+        def split_alphas(turn, part):
+            lo, hi = slot_range(turn + 1, SLOTS)
             if lo == hi:
                 return
             if part == 0:
-                alpha_parts[step + 1] = small.tile([P, ROUNDS, PARTS], BF16, name="alpha_part", tag="alpha_part")
-            parts = alpha_parts[step + 1][:, lo:hi]
-            split(parts[:, :, 0], parts[:, :, 1], alphas[step + 1][:, 0, lo:hi], part)
+                alpha_parts[turn + 1] = small.tile([P, SLOTS, KINDS, PARTS], BF16, name="alpha_part", tag="alpha_part")
+            parts = alpha_parts[turn + 1][:, lo:hi]
+            split(parts[:, :, :, 0], parts[:, :, :, 1], alphas[turn + 1][:, lo:hi, :], part)
 
-        def spread_betas(step, half):
-            r = ROUNDS - 1
-            if not is_image(image_in_round(step, r)):
+        def last_turn_and_slot(b):
+            pair, e = divmod(b, PAIR)
+            return pair + LEAD + ROUNDS - 1, (ROUNDS - 1) * PAIR + e
+
+        def spread_betas(b, half):
+            if not is_image(b):
                 return
+            turn, slot = last_turn_and_slot(b)
             spreads[half] = psum_t.tile([P, CHUNKS_PER_BANK, P], F32, name="spread", tag="flip")
             for q in range(CHUNKS_PER_BANK):
                 j = half * CHUNKS_PER_BANK + q
-                nc.tensor.transpose(spreads[half][:, q, :], betas[step][:, r, j : j + 1].to_broadcast([P, P]), ident[:])
+                nc.tensor.transpose(
+                    spreads[half][:, q, :], betas[turn][:, slot, j : j + 1].to_broadcast([P, P]), ident[:]
+                )
 
-        def scale_and_store(step, half):
-            r = ROUNDS - 1
-            b = image_in_round(step, r)
+        def scale_and_store(b, half):
             if not is_image(b):
                 return
+            turn, slot = last_turn_and_slot(b)
             if half == 0:
                 results[b] = sk.tile([P, PIXELS], F32, name="result", tag="result")
             nc.vector.scalar_tensor_tensor(
                 out=results[b][:, half_cols(half)],
                 in0=kern[b][:, half_cols(half)],
-                scalar=alphas[step][:, 0, r : r + 1],
+                scalar=alphas[turn][:, slot, 0:1],
                 in1=spreads[half][:].rearrange("p q n -> p (q n)"),
                 op0=ALU.mult,
                 op1=ALU.mult,
@@ -433,50 +439,67 @@ def tile_salad_pa_t_kernel(tc, x, Ws1, bs1, Ws2, out):
             if half == HALVES - 1:
                 nc.sync.dma_start(out=out[b], in_=results[b][:])
 
-        for s in range(IMAGES + 5 + ROUNDS - 1):
-            grouped, hidden, scored, exped = s - 1, s - 2, s - 3, s - 4
+        STEPS_TO_RESULT = (LEAD + ROUNDS - 1) * PAIR + 1
+        for s in range(IMAGES + STEPS_TO_RESULT):
+            grouped, hidden, scored, exped, finished = s - 1, s - 2, s - 3, s - 4, s - STEPS_TO_RESULT
+            turn, phase = divmod(s, PAIR)
+            columns = phase == 0
+
+            def sums_of(first, last):
+                for slot in range(first, last):
+                    if columns:
+                        column_sums(turn, slot)
+                    elif slot < ROWS:
+                        row_sums(turn, slot)
+
             load_image(s)
-            prepare_sums(s)
+            if not columns:
+                prepare_sums(turn)
             regroup_hidden(scored, 1)
             hidden_pass(hidden, 0)
             regroup_image(grouped, 0)
-            column_sums(s, 0)
+            sums_of(0, 2)
             quantise_image(hidden, 1)
             hidden_pass(hidden, 1)
-            column_sums(s, 1)
+            sums_of(2, 4)
             hidden_pass(hidden, 2)
             regroup_image(grouped, 1)
-            column_sums(s, 2)
-            sum_columns(s)
+            sums_of(4, 6)
+            if columns:
+                sum_columns(turn)
+            else:
+                sum_rows(turn)
             low_parts(exped)
-            add_dustbin(s)
+            if columns:
+                invert_columns(turn)
+            else:
+                invert_rows(turn)
             quantise_hidden(scored, 1)
-            invert_columns(s)
+            if columns:
+                split_betas(turn, 0)
+            else:
+                split_alphas(turn, 0)
             hidden_pass(hidden, 3)
             cluster_scores(scored)
             regroup_image(grouped, 2)
-            split_betas(s, 0)
+            if columns:
+                split_betas(turn, 1)
+            else:
+                split_alphas(turn, 1)
             hidden_pass(hidden, 4)
             flip_kernel(exped)
             half_tops(scored, 0)
-            split_betas(s, 1)
             half_tops(scored, 1)
-            spread_betas(s, 0)
+            spread_betas(finished, 0)
             hidden_pass(hidden, 5)
-            row_sums(s, 0)
             regroup_image(grouped, 3)
             negated_tops(scored)
             hidden_pass(hidden, 6)
-            row_sums(s, 1)
-            spread_betas(s, 1)
+            spread_betas(finished, 1)
             quantise_image(grouped, 0)
-            sum_rows(s)
-            scale_and_store(s, 0)
-            invert_rows(s)
-            scale_and_store(s, 1)
-            split_alphas(s, 0)
+            scale_and_store(finished, 0)
+            scale_and_store(finished, 1)
             regroup_hidden(hidden, 0)
-            split_alphas(s, 1)
             quantise_hidden(hidden, 0)
             hidden_pass(hidden, 7)
             exponentials(scored)

@@ -23,9 +23,7 @@ CHUNKS = PIXELS // P
 CHUNKS_PER_BANK = BANK // P
 ROUNDS = 3
 RUN = 4
-PIECES = 4
-SCALAR_PIECES = 2
-PIECE = PIXELS // PIECES
+SCALAR_PIXELS = 256
 PAIR = 2
 PAIRS = IMAGES // PAIR
 LEAD = 3
@@ -122,28 +120,27 @@ def tile_salad_pa_t_kernel(tc, x, Ws1, bs1, Ws2, out):
             x_raw[b] = xs.tile([P, PACK, PIXELS], BF16, name="x_raw", tag="x_raw", bufs=3)
             nc.sync.dma_start(out=x_raw[b][:], in_=x[b].rearrange("(p j) h w -> p j (h w)", j=PACK))
 
-        def regroup_image(b, piece):
+        def regroup_image(b, engine):
             if not is_image(b):
                 return
-            if piece == 0:
+            if b not in x_grouped:
                 x_grouped[b] = xs.tile([P, PIXELS, PACK], BF16, name="x_grouped", tag="x_grouped", align_bytes=64)
-            cols = slice(piece * PIECE, (piece + 1) * PIECE)
+            cols = slice(0, SCALAR_PIXELS) if engine == "scalar" else slice(SCALAR_PIXELS, PIXELS)
             dst, src = regrouped(x_grouped[b][:, cols, :], x_raw[b][:, :, cols])
-            if piece < SCALAR_PIECES:
+            if engine == "scalar":
                 nc.scalar.copy(out=dst, in_=src)
             else:
                 nc.vector.tensor_copy(out=dst, in_=src)
 
-        def quantise_image(b, half):
+        def quantise_image(b):
             if not is_image(b):
                 return
-            if half == 0:
-                x_codes[b] = xs.tile([P, PIXELS], U32, name="x_codes", tag="x_codes", align_bytes=64)
-                x_scales[b] = xs.tile([P, PIXELS], U8, name="x_scales", tag="x_scales", align_bytes=64)
+            x_codes[b] = xs.tile([P, PIXELS], U32, name="x_codes", tag="x_codes", align_bytes=64)
+            x_scales[b] = xs.tile([P, PIXELS], U8, name="x_scales", tag="x_scales", align_bytes=64)
             nc.vector.quantize_mx(
-                out=x_codes[b][:, half_cols(half)].bitcast(FP8X4),
-                scales=x_scales[b][:, half_cols(half)],
-                in_=x_grouped[b][:, half_cols(half), :].rearrange("p n j -> p (n j)"),
+                out=x_codes[b][:].bitcast(FP8X4),
+                scales=x_scales[b][:],
+                in_=x_grouped[b][:].rearrange("p n j -> p (n j)"),
             )
 
         def hidden_pass(b, k):
@@ -269,7 +266,14 @@ def tile_salad_pa_t_kernel(tc, x, Ws1, bs1, Ws2, out):
 
         COLUMN_AT = 0
         ROW_AT = COLUMN_AT + SLOTS * CHUNKS * WIDTH
-        SUMS = ROW_AT + ROWS * KINDS * WIDTH
+        ROW_WIDTH = CHUNKS * PARTS
+        SUMS = ROW_AT + ROWS * KINDS * ROW_WIDTH
+
+        def columns_of(turn, lo, hi):
+            return sums[turn][:, COLUMN_AT:ROW_AT].rearrange("p (r j c) -> p r j c", j=CHUNKS, c=WIDTH)[:, lo:hi]
+
+        def rows_of(turn, lo, hi):
+            return sums[turn][:, ROW_AT:SUMS].rearrange("p (r k c) -> p r k c", k=KINDS, c=ROW_WIDTH)[:, lo:hi]
 
         def image_in_slot(turn, slot):
             r, e = divmod(slot, PAIR)
@@ -286,32 +290,36 @@ def tile_salad_pa_t_kernel(tc, x, Ws1, bs1, Ws2, out):
             else:
                 nc.vector.tensor_tensor(out=low, in0=values, in1=high, op=ALU.subtract)
 
-        def repeated(parts, times=REPEAT):
-            return parts.unsqueeze(1).to_broadcast([P, times, PARTS])
+        def repeated(parts):
+            return parts.unsqueeze(1).to_broadcast([P, REPEAT, PARTS])
+
+        def open_column_sums(turn):
+            lo, hi = slot_range(turn, SLOTS)
+            if lo == hi:
+                return
+            sums[turn] = psum_v.tile([P, SUMS], F32, name="sums", tag="sums")
+            nc.tensor.matmul(
+                out=columns_of(turn, lo, hi).rearrange("p r j c -> p r (j c)"),
+                lhsT=row_mean[:],
+                rhs=alpha_parts[turn][:, lo:hi, 1, :].unsqueeze(2).to_broadcast([P, hi - lo, CHUNKS * REPEAT, PARTS]),
+                start=True,
+                stop=False,
+            )
 
         def column_sums(turn, slot):
             b = image_in_slot(turn, slot)
             if not is_image(b):
                 return
-            if turn not in sums:
-                sums[turn] = psum_v.tile([P, SUMS], F32, name="sums", tag="sums")
-            at = COLUMN_AT + slot * CHUNKS * WIDTH
-            nc.tensor.matmul(
-                out=sums[turn][:, at : at + CHUNKS * WIDTH],
-                lhsT=row_mean[:],
-                rhs=repeated(alpha_parts[turn][:, slot, 1, :], CHUNKS * REPEAT),
-                start=True,
-                stop=False,
-            )
+            last_slot = slot == slot_range(turn, SLOTS)[1] - 1
             for j in range(CHUNKS):
                 cols = slice(j * P, (j + 1) * P)
                 for part, rows in enumerate((high_parts(b), kern_lo[b][:])):
                     nc.tensor.matmul(
-                        out=sums[turn][:, at + j * WIDTH : at + (j + 1) * WIDTH],
+                        out=columns_of(turn, slot, slot + 1)[:, 0, j, :],
                         lhsT=rows[:, cols],
                         rhs=repeated(alpha_parts[turn][:, slot, 0, :]),
                         start=False,
-                        stop=(j == CHUNKS - 1 and part == PARTS - 1),
+                        stop=(last_slot and j == CHUNKS - 1 and part == PARTS - 1),
                     )
 
         def sum_columns(turn):
@@ -321,9 +329,7 @@ def tile_salad_pa_t_kernel(tc, x, Ws1, bs1, Ws2, out):
             betas[turn] = small.tile([P, SLOTS, CHUNKS], F32, name="beta", tag="beta")
             nc.vector.reduce_sum(
                 out=betas[turn][:, lo:hi, :],
-                in_=sums[turn][:, COLUMN_AT:ROW_AT].rearrange("p (r j c) -> p r j c", j=CHUNKS, c=WIDTH)[
-                    :, lo:hi, :, 0:PARTS
-                ],
+                in_=columns_of(turn, lo, hi)[:, :, :, 0:PARTS],
                 axis=AX.X,
             )
 
@@ -346,25 +352,27 @@ def tile_salad_pa_t_kernel(tc, x, Ws1, bs1, Ws2, out):
             b = image_in_slot(turn, slot)
             if not is_image(b):
                 return
-            at = ROW_AT + slot * KINDS * WIDTH
             for j in range(CHUNKS):
                 for part in range(PARTS):
                     nc.tensor.matmul(
-                        out=sums[turn][:, at : at + WIDTH],
+                        out=rows_of(turn, slot, slot + 1)[:, 0, 0, j * PARTS : (j + 1) * PARTS],
                         lhsT=kern_t[b][:, part, j, :],
-                        rhs=repeated(beta_parts[turn][:, slot, j, :]),
-                        start=(j == 0 and part == 0),
-                        stop=(j == CHUNKS - 1 and part == PARTS - 1),
+                        rhs=beta_parts[turn][:, slot, j, :],
+                        start=(part == 0),
+                        stop=(part == PARTS - 1),
                     )
-            at = at + WIDTH
-            for j in range(CHUNKS):
-                nc.tensor.matmul(
-                    out=sums[turn][:, at : at + WIDTH],
-                    lhsT=pixel_mean[:],
-                    rhs=repeated(beta_parts[turn][:, slot, j, :]),
-                    start=(j == 0),
-                    stop=(j == CHUNKS - 1),
-                )
+
+        def dustbin_sums(turn):
+            lo, hi = slot_range(turn, ROWS)
+            if lo == hi:
+                return
+            nc.tensor.matmul(
+                out=rows_of(turn, lo, hi)[:, :, 1, :],
+                lhsT=pixel_mean[:],
+                rhs=beta_parts[turn][:, lo:hi].rearrange("p r j c -> p r (j c)"),
+                start=True,
+                stop=True,
+            )
 
         def prepare_sums(turn):
             lo, hi = slot_range(turn + 1, SLOTS)
@@ -385,9 +393,7 @@ def tile_salad_pa_t_kernel(tc, x, Ws1, bs1, Ws2, out):
                 return
             nc.vector.reduce_sum(
                 out=belows[turn][:, old:hi, 0:KINDS],
-                in_=sums[turn][:, ROW_AT:SUMS].rearrange("p (r k c) -> p r k c", k=KINDS, c=WIDTH)[
-                    :, old - OLD : hi - OLD, :, 0:PARTS
-                ],
+                in_=rows_of(turn, old - OLD, hi - OLD),
                 axis=AX.X,
             )
 
@@ -457,13 +463,15 @@ def tile_salad_pa_t_kernel(tc, x, Ws1, bs1, Ws2, out):
                 prepare_sums(turn)
             regroup_hidden(scored, 1)
             hidden_pass(hidden, 0)
-            regroup_image(grouped, 0)
+            regroup_image(grouped, "scalar")
+            if columns:
+                open_column_sums(turn)
+            else:
+                dustbin_sums(turn)
             sums_of(0, 2)
-            quantise_image(hidden, 1)
             hidden_pass(hidden, 1)
             sums_of(2, 4)
             hidden_pass(hidden, 2)
-            regroup_image(grouped, 1)
             sums_of(4, 6)
             if columns:
                 sum_columns(turn)
@@ -481,7 +489,7 @@ def tile_salad_pa_t_kernel(tc, x, Ws1, bs1, Ws2, out):
                 split_alphas(turn, 0)
             hidden_pass(hidden, 3)
             cluster_scores(scored)
-            regroup_image(grouped, 2)
+            regroup_image(grouped, "vector")
             if columns:
                 split_betas(turn, 1)
             else:
@@ -492,11 +500,10 @@ def tile_salad_pa_t_kernel(tc, x, Ws1, bs1, Ws2, out):
             half_tops(scored, 1)
             spread_betas(finished, 0)
             hidden_pass(hidden, 5)
-            regroup_image(grouped, 3)
             negated_tops(scored)
             hidden_pass(hidden, 6)
             spread_betas(finished, 1)
-            quantise_image(grouped, 0)
+            quantise_image(grouped)
             scale_and_store(finished, 0)
             scale_and_store(finished, 1)
             regroup_hidden(hidden, 0)

@@ -24,14 +24,13 @@ CHUNKS_PER_BANK = BANK // P
 ROUNDS = 3
 RUN = 4
 SCALAR_PIXELS = 256
-PAIR = 2
-PAIRS = IMAGES // PAIR
-LEAD = 3
-SLOTS = ROUNDS * PAIR
-OLD = PAIR
-ROWS = SLOTS - PAIR
+STEPS_TO_ROUNDS = 5
+PAIRED = IMAGES - 2
+STREAMS = ([(b, b + 1) for b in range(0, PAIRED, 2)], [(IMAGES - 2,)], [(IMAGES - 1,)])
+X_AHEAD = 1
 PARTS = 2
 REPEAT = 4
+ROW_WIDTH = PIXELS // P * PARTS
 KINDS = 2
 SLOT = 8
 WIDTH = REPEAT * PARTS
@@ -82,7 +81,7 @@ def tile_salad_pa_t_kernel(tc, x, Ws1, bs1, Ws2, out):
             flipped = psum_t.tile([P, CHUNKS_PER_BANK, P], F32, name="flipped", tag="flip")
             for u in range(2):
                 nc.tensor.transpose(flipped[:, u, :], words[:, u, :], ident[:])
-            nc.vector.tensor_copy(
+            nc.scalar.copy(
                 out=grouped.bitcast(F32).rearrange("p (r u) -> p r u", u=2),
                 in_=flipped[:, 0:2, :].rearrange("p u r -> p r u"),
             )
@@ -135,8 +134,8 @@ def tile_salad_pa_t_kernel(tc, x, Ws1, bs1, Ws2, out):
         def quantise_image(b):
             if not is_image(b):
                 return
-            x_codes[b] = xs.tile([P, PIXELS], U32, name="x_codes", tag="x_codes", align_bytes=64)
-            x_scales[b] = xs.tile([P, PIXELS], U8, name="x_scales", tag="x_scales", align_bytes=64)
+            x_codes[b] = xs.tile([P, PIXELS], U32, name="x_codes", tag="x_codes", bufs=2 + X_AHEAD, align_bytes=64)
+            x_scales[b] = xs.tile([P, PIXELS], U8, name="x_scales", tag="x_scales", bufs=2 + X_AHEAD, align_bytes=64)
             nc.vector.quantize_mx(
                 out=x_codes[b][:].bitcast(FP8X4),
                 scales=x_scales[b][:],
@@ -224,7 +223,7 @@ def tile_salad_pa_t_kernel(tc, x, Ws1, bs1, Ws2, out):
         def exponentials(b):
             if not is_image(b):
                 return
-            kern[b] = sk.tile([P, PIXELS], F32, name="kern", tag="kern", bufs=10)
+            kern[b] = sk.tile([P, PIXELS], F32, name="kern", tag="kern", bufs=9)
             first_sums[b] = small.tile([P, HALVES], F32, name="first_sum", tag="first_sum")
             for half in range(HALVES):
                 nc.scalar.activation(
@@ -245,44 +244,48 @@ def tile_salad_pa_t_kernel(tc, x, Ws1, bs1, Ws2, out):
             kern_lo[b] = sk.tile([P, PIXELS], BF16, name="kern_lo", tag="kern_lo", bufs=8)
             nc.vector.tensor_tensor(out=kern_lo[b][:], in0=kern[b][:], in1=high_parts(b), op=ALU.subtract)
 
-        def flip_kernel(b):
+        def flip_high(b):
             if not is_image(b):
                 return
             kern_t[b] = sk.tile([P, PARTS, CHUNKS, P], BF16, name="kern_t", tag="kern_t", bufs=7)
-            flipped_hi = psum_t.tile([P, CHUNKS, P], BF16, name="flipped_hi", tag="flip")
+            flipped = psum_t.tile([P, CHUNKS, P], BF16, name="flipped_hi", tag="flip")
             for j in range(CHUNKS):
                 nc.tensor.matmul(
-                    out=flipped_hi[:, j, :],
+                    out=flipped[:, j, :],
                     lhsT=high_parts(b)[:, j * P : (j + 1) * P],
                     rhs=ident_bf[:],
                     start=True,
                     stop=True,
                 )
-            nc.scalar.copy(out=kern_t[b][:, 0], in_=flipped_hi[:])
-            flipped_lo = psum_t.tile([P, CHUNKS, P], BF16, name="flipped_lo", tag="flip")
+            nc.scalar.copy(out=kern_t[b][:, 0], in_=flipped[:])
+
+        def flip_low(b):
+            if not is_image(b):
+                return
+            flipped = psum_t.tile([P, CHUNKS, P], BF16, name="flipped_lo", tag="flip")
             for j in range(CHUNKS):
-                nc.tensor.transpose(flipped_lo[:, j, :], kern_lo[b][:, j * P : (j + 1) * P], ident_bf[:])
-            nc.scalar.copy(out=kern_t[b][:, 1], in_=flipped_lo[:])
+                nc.tensor.transpose(flipped[:, j, :], kern_lo[b][:, j * P : (j + 1) * P], ident_bf[:])
+            nc.scalar.copy(out=kern_t[b][:, 1], in_=flipped[:])
 
-        COLUMN_AT = 0
-        ROW_AT = COLUMN_AT + SLOTS * CHUNKS * WIDTH
-        ROW_WIDTH = CHUNKS * PARTS
-        SUMS = ROW_AT + ROWS * KINDS * ROW_WIDTH
+        streams = []
+        for groups in STREAMS:
+            streams.append((len(streams), groups, groups[0][-1] + STEPS_TO_ROUNDS))
 
-        def columns_of(turn, lo, hi):
-            return sums[turn][:, COLUMN_AT:ROW_AT].rearrange("p (r j c) -> p r j c", j=CHUNKS, c=WIDTH)[:, lo:hi]
+        def image_in_slot(stream, turn, slot):
+            groups = stream[1]
+            r, e = divmod(slot, len(groups[0]))
+            return groups[turn - r][e] if 0 <= turn - r < len(groups) else -1
 
-        def rows_of(turn, lo, hi):
-            return sums[turn][:, ROW_AT:SUMS].rearrange("p (r k c) -> p r k c", k=KINDS, c=ROW_WIDTH)[:, lo:hi]
+        def slots_of(stream, rounds):
+            return rounds * len(stream[1][0])
 
-        def image_in_slot(turn, slot):
-            r, e = divmod(slot, PAIR)
-            pair = turn - LEAD - r
-            return pair * PAIR + e if 0 <= pair < PAIRS else -1
-
-        def slot_range(turn, slots):
-            held = [slot for slot in range(slots) if is_image(image_in_slot(turn, slot))]
+        def slot_range(stream, turn, slots):
+            held = [slot for slot in range(slots) if is_image(image_in_slot(stream, turn, slot))]
             return (held[0], held[-1] + 1) if held else (0, 0)
+
+        def small_tile(stream, name, shape, dtype):
+            tag = name + str(stream[0])
+            return small.tile(shape, dtype, name=tag, tag=tag)
 
         def split(high, low, values, part):
             if part == 0:
@@ -290,222 +293,268 @@ def tile_salad_pa_t_kernel(tc, x, Ws1, bs1, Ws2, out):
             else:
                 nc.vector.tensor_tensor(out=low, in0=values, in1=high, op=ALU.subtract)
 
-        def repeated(parts):
-            return parts.unsqueeze(1).to_broadcast([P, REPEAT, PARTS])
+        def columns_of(stream, turn, lo, hi):
+            end = slots_of(stream, ROUNDS) * CHUNKS * WIDTH
+            return sums[stream[0], turn][:, 0:end].rearrange("p (r j c) -> p r j c", j=CHUNKS, c=WIDTH)[:, lo:hi]
 
-        def open_column_sums(turn):
-            lo, hi = slot_range(turn, SLOTS)
+        def rows_of(stream, turn, lo, hi):
+            start = slots_of(stream, ROUNDS) * CHUNKS * WIDTH
+            end = start + slots_of(stream, ROUNDS - 1) * KINDS * ROW_WIDTH
+            return sums[stream[0], turn][:, start:end].rearrange("p (r k c) -> p r k c", k=KINDS, c=ROW_WIDTH)[:, lo:hi]
+
+        def slots_of_piece(stream, lo, hi, piece):
+            size = len(stream[1][0])
+            return [slot for slot in range(lo, hi) if piece is None or slot // size == piece]
+
+        def column_sums(stream, turn, piece):
+            lo, hi = slot_range(stream, turn, slots_of(stream, ROUNDS))
             if lo == hi:
                 return
-            sums[turn] = psum_v.tile([P, SUMS], F32, name="sums", tag="sums")
-            nc.tensor.matmul(
-                out=columns_of(turn, lo, hi).rearrange("p r j c -> p r (j c)"),
-                lhsT=row_mean[:],
-                rhs=alpha_parts[turn][:, lo:hi, 1, :].unsqueeze(2).to_broadcast([P, hi - lo, CHUNKS * REPEAT, PARTS]),
-                start=True,
-                stop=False,
-            )
+            parts = alpha_parts[stream[0], turn]
+            if (stream[0], turn) not in sums:
+                if stream[0] == 0:
+                    tile = psum_v.tile([P, BANK], F32, name="sums", tag="sums")
+                else:
+                    tile = psum_z.tile([P, BANK], F32, name="sums_z", tag="z")
+                sums[stream[0], turn] = tile
+                nc.tensor.matmul(
+                    out=columns_of(stream, turn, lo, hi).rearrange("p r j c -> p r (j c)"),
+                    lhsT=row_mean[:],
+                    rhs=parts[:, lo:hi, 1, :].unsqueeze(2).to_broadcast([P, hi - lo, CHUNKS * REPEAT, PARTS]),
+                    start=True,
+                    stop=False,
+                )
+            for slot in slots_of_piece(stream, lo, hi, piece):
+                b = image_in_slot(stream, turn, slot)
+                for j in range(CHUNKS):
+                    cols = slice(j * P, (j + 1) * P)
+                    for part, rows in enumerate((high_parts(b), kern_lo[b][:])):
+                        nc.tensor.matmul(
+                            out=columns_of(stream, turn, slot, slot + 1)[:, 0, j, :],
+                            lhsT=rows[:, cols],
+                            rhs=parts[:, slot, 0, :].unsqueeze(1).to_broadcast([P, REPEAT, PARTS]),
+                            start=False,
+                            stop=(slot == hi - 1 and j == CHUNKS - 1 and part == PARTS - 1),
+                        )
 
-        def column_sums(turn, slot):
-            b = image_in_slot(turn, slot)
-            if not is_image(b):
-                return
-            last_slot = slot == slot_range(turn, SLOTS)[1] - 1
-            for j in range(CHUNKS):
-                cols = slice(j * P, (j + 1) * P)
-                for part, rows in enumerate((high_parts(b), kern_lo[b][:])):
-                    nc.tensor.matmul(
-                        out=columns_of(turn, slot, slot + 1)[:, 0, j, :],
-                        lhsT=rows[:, cols],
-                        rhs=repeated(alpha_parts[turn][:, slot, 0, :]),
-                        start=False,
-                        stop=(last_slot and j == CHUNKS - 1 and part == PARTS - 1),
-                    )
-
-        def sum_columns(turn):
-            lo, hi = slot_range(turn, SLOTS)
+        def sum_columns(stream, turn):
+            slots = slots_of(stream, ROUNDS)
+            lo, hi = slot_range(stream, turn, slots)
             if lo == hi:
                 return
-            betas[turn] = small.tile([P, SLOTS, CHUNKS], F32, name="beta", tag="beta")
+            betas[stream[0], turn] = small_tile(stream, "beta", [P, slots, CHUNKS], F32)
             nc.vector.reduce_sum(
-                out=betas[turn][:, lo:hi, :],
-                in_=columns_of(turn, lo, hi)[:, :, :, 0:PARTS],
+                out=betas[stream[0], turn][:, lo:hi, :],
+                in_=columns_of(stream, turn, lo, hi)[:, :, :, 0:PARTS],
                 axis=AX.X,
             )
 
-        def invert_columns(turn):
-            lo, hi = slot_range(turn, SLOTS)
+        def invert_columns(stream, turn):
+            lo, hi = slot_range(stream, turn, slots_of(stream, ROUNDS))
             if lo == hi:
                 return
-            nc.vector.reciprocal(out=betas[turn][:, lo:hi, :], in_=betas[turn][:, lo:hi, :])
+            beta = betas[stream[0], turn][:, lo:hi, :]
+            nc.vector.reciprocal(out=beta, in_=beta)
 
-        def split_betas(turn, part):
-            lo, hi = slot_range(turn, ROWS)
+        def split_betas(stream, turn, part):
+            slots = slots_of(stream, ROUNDS - 1)
+            lo, hi = slot_range(stream, turn, slots)
             if lo == hi:
                 return
             if part == 0:
-                beta_parts[turn] = small.tile([P, ROWS, CHUNKS, PARTS], BF16, name="beta_part", tag="beta_part")
-            parts = beta_parts[turn][:, lo:hi]
-            split(parts[:, :, :, 0], parts[:, :, :, 1], betas[turn][:, lo:hi, :], part)
+                beta_parts[stream[0], turn] = small_tile(stream, "beta_part", [P, slots, CHUNKS, PARTS], BF16)
+            parts = beta_parts[stream[0], turn][:, lo:hi]
+            split(parts[:, :, :, 0], parts[:, :, :, 1], betas[stream[0], turn][:, lo:hi, :], part)
 
-        def row_sums(turn, slot):
-            b = image_in_slot(turn, slot)
-            if not is_image(b):
-                return
-            for j in range(CHUNKS):
-                for part in range(PARTS):
-                    nc.tensor.matmul(
-                        out=rows_of(turn, slot, slot + 1)[:, 0, 0, j * PARTS : (j + 1) * PARTS],
-                        lhsT=kern_t[b][:, part, j, :],
-                        rhs=beta_parts[turn][:, slot, j, :],
-                        start=(part == 0),
-                        stop=(part == PARTS - 1),
-                    )
-
-        def dustbin_sums(turn):
-            lo, hi = slot_range(turn, ROWS)
+        def row_sums(stream, turn, piece):
+            lo, hi = slot_range(stream, turn, slots_of(stream, ROUNDS - 1))
             if lo == hi:
                 return
-            nc.tensor.matmul(
-                out=rows_of(turn, lo, hi)[:, :, 1, :],
-                lhsT=pixel_mean[:],
-                rhs=beta_parts[turn][:, lo:hi].rearrange("p r j c -> p r (j c)"),
-                start=True,
-                stop=True,
-            )
-
-        def prepare_sums(turn):
-            lo, hi = slot_range(turn + 1, SLOTS)
-            if lo == hi:
-                return
-            belows[turn] = small.tile([P, SLOTS, SLOT], F32, name="below", tag="below")
-            nc.gpsimd.memset(belows[turn][:], 1.0)
-            for slot in range(lo, min(hi, OLD)):
-                halves = first_sums[image_in_slot(turn + 1, slot)]
-                nc.gpsimd.tensor_tensor(
-                    out=belows[turn][:, slot, 0:1], in0=halves[:, 0:1], in1=halves[:, 1:2], op=ALU.add
+            parts = beta_parts[stream[0], turn]
+            if not piece:
+                nc.tensor.matmul(
+                    out=rows_of(stream, turn, lo, hi)[:, :, 1, :],
+                    lhsT=pixel_mean[:],
+                    rhs=parts[:, lo:hi].rearrange("p r j c -> p r (j c)"),
+                    start=True,
+                    stop=True,
                 )
+            for slot in slots_of_piece(stream, lo, hi, piece):
+                b = image_in_slot(stream, turn, slot)
+                for j in range(CHUNKS):
+                    for part in range(PARTS):
+                        nc.tensor.matmul(
+                            out=rows_of(stream, turn, slot, slot + 1)[:, 0, 0, j * PARTS : (j + 1) * PARTS],
+                            lhsT=kern_t[b][:, part, j, :],
+                            rhs=parts[:, slot, j, :],
+                            start=(part == 0),
+                            stop=(part == PARTS - 1),
+                        )
 
-        def sum_rows(turn):
-            lo, hi = slot_range(turn + 1, SLOTS)
-            old = max(lo, OLD)
+        def prepare_sums(stream, turn):
+            slots = slots_of(stream, ROUNDS)
+            lo, hi = slot_range(stream, turn + 1, slots)
+            if lo == hi:
+                return
+            below = small_tile(stream, "below", [P, slots, SLOT], F32)
+            belows[stream[0], turn] = below
+            if lo < slots_of(stream, 1):
+                nc.gpsimd.memset(below[:], 1.0)
+            for slot in range(lo, min(hi, slots_of(stream, 1))):
+                halves = first_sums[image_in_slot(stream, turn + 1, slot)]
+                nc.gpsimd.tensor_tensor(out=below[:, slot, 0:1], in0=halves[:, 0:1], in1=halves[:, 1:2], op=ALU.add)
+
+        def sum_rows(stream, turn):
+            lo, hi = slot_range(stream, turn + 1, slots_of(stream, ROUNDS))
+            new = slots_of(stream, 1)
+            old = max(lo, new)
             if old >= hi:
                 return
             nc.vector.reduce_sum(
-                out=belows[turn][:, old:hi, 0:KINDS],
-                in_=rows_of(turn, old - OLD, hi - OLD),
+                out=belows[stream[0], turn][:, old:hi, 0:KINDS],
+                in_=rows_of(stream, turn, old - new, hi - new),
                 axis=AX.X,
             )
 
-        def invert_rows(turn):
-            lo, hi = slot_range(turn + 1, SLOTS)
+        def invert_rows(stream, turn):
+            slots = slots_of(stream, ROUNDS)
+            lo, hi = slot_range(stream, turn + 1, slots)
             if lo == hi:
                 return
-            alphas[turn + 1] = small.tile([P, SLOTS, KINDS], F32, name="alpha", tag="alpha")
-            nc.vector.reciprocal(out=alphas[turn + 1][:, lo:hi, :], in_=belows[turn][:, lo:hi, 0:KINDS])
+            alphas[stream[0], turn + 1] = small_tile(stream, "alpha", [P, slots, KINDS], F32)
+            nc.vector.reciprocal(
+                out=alphas[stream[0], turn + 1][:, lo:hi, :], in_=belows[stream[0], turn][:, lo:hi, 0:KINDS]
+            )
 
-        def split_alphas(turn, part):
-            lo, hi = slot_range(turn + 1, SLOTS)
+        def split_alphas(stream, turn, part):
+            slots = slots_of(stream, ROUNDS)
+            lo, hi = slot_range(stream, turn + 1, slots)
             if lo == hi:
                 return
             if part == 0:
-                alpha_parts[turn + 1] = small.tile([P, SLOTS, KINDS, PARTS], BF16, name="alpha_part", tag="alpha_part")
-            parts = alpha_parts[turn + 1][:, lo:hi]
-            split(parts[:, :, :, 0], parts[:, :, :, 1], alphas[turn + 1][:, lo:hi, :], part)
+                alpha_parts[stream[0], turn + 1] = small_tile(stream, "alpha_part", [P, slots, KINDS, PARTS], BF16)
+            parts = alpha_parts[stream[0], turn + 1][:, lo:hi]
+            split(parts[:, :, :, 0], parts[:, :, :, 1], alphas[stream[0], turn + 1][:, lo:hi, :], part)
 
-        def last_turn_and_slot(b):
-            pair, e = divmod(b, PAIR)
-            return pair + LEAD + ROUNDS - 1, (ROUNDS - 1) * PAIR + e
+        def halves_of_step(s):
+            found = []
+            for stream in reversed(streams):
+                turn, kind = divmod(s - stream[2], 2)
+                found.append((stream, turn, kind))
+            return found
+
+        def big_sums(stream, turn, kind, piece=None):
+            if kind == 0:
+                column_sums(stream, turn, piece)
+            else:
+                if not piece:
+                    prepare_sums(stream, turn)
+                row_sums(stream, turn, piece)
+
+        def small_op(stream, turn, kind, part):
+            if part == 0:
+                (sum_columns, sum_rows)[kind](stream, turn)
+            elif part == 1:
+                (invert_columns, invert_rows)[kind](stream, turn)
+            else:
+                (split_betas, split_alphas)[kind](stream, turn, part - 2)
+
+        last_places = {}
+        finals = {}
+        for stream in streams:
+            for g, group in enumerate(stream[1]):
+                for e, b in enumerate(group):
+                    last_turn = g + ROUNDS - 1
+                    last_places[b] = (stream[0], last_turn, (ROUNDS - 1) * len(group) + e)
+                    after = e + 1 if len(group) > 1 else 0
+                    finals.setdefault(stream[2] + 2 * last_turn + after, []).append(b)
 
         def spread_betas(b, half):
-            if not is_image(b):
-                return
-            turn, slot = last_turn_and_slot(b)
-            spreads[half] = psum_t.tile([P, CHUNKS_PER_BANK, P], F32, name="spread", tag="flip")
+            number, turn, slot = last_places[b]
+            spreads[b, half] = psum_t.tile([P, CHUNKS_PER_BANK, P], F32, name="spread", tag="flip")
             for q in range(CHUNKS_PER_BANK):
                 j = half * CHUNKS_PER_BANK + q
                 nc.tensor.transpose(
-                    spreads[half][:, q, :], betas[turn][:, slot, j : j + 1].to_broadcast([P, P]), ident[:]
+                    spreads[b, half][:, q, :], betas[number, turn][:, slot, j : j + 1].to_broadcast([P, P]), ident[:]
                 )
 
         def scale_and_store(b, half):
-            if not is_image(b):
-                return
-            turn, slot = last_turn_and_slot(b)
+            number, turn, slot = last_places[b]
             if half == 0:
-                results[b] = sk.tile([P, PIXELS], F32, name="result", tag="result")
+                results[b] = sk.tile([P, PIXELS], F32, name="result", tag="result", bufs=4)
+            cols = half_cols(half)
             nc.vector.scalar_tensor_tensor(
-                out=results[b][:, half_cols(half)],
-                in0=kern[b][:, half_cols(half)],
-                scalar=alphas[turn][:, slot, 0:1],
-                in1=spreads[half][:].rearrange("p q n -> p (q n)"),
+                out=results[b][:, cols],
+                in0=kern[b][:, cols],
+                scalar=alphas[number, turn][:, slot, 0:1],
+                in1=spreads[b, half][:].rearrange("p q n -> p (q n)"),
                 op0=ALU.mult,
                 op1=ALU.mult,
             )
-            if half == HALVES - 1:
-                nc.sync.dma_start(out=out[b], in_=results[b][:])
+            nc.sync.dma_start(out=out[b][:, cols], in_=results[b][:, cols])
 
-        STEPS_TO_RESULT = (LEAD + ROUNDS - 1) * PAIR + 1
-        for s in range(IMAGES + STEPS_TO_RESULT):
-            grouped, hidden, scored, exped, finished = s - 1, s - 2, s - 3, s - 4, s - STEPS_TO_RESULT
-            turn, phase = divmod(s, PAIR)
-            columns = phase == 0
-
-            def sums_of(first, last):
-                for slot in range(first, last):
-                    if columns:
-                        column_sums(turn, slot)
-                    elif slot < ROWS:
-                        row_sums(turn, slot)
-
-            load_image(s)
-            if not columns:
-                prepare_sums(turn)
+        for b in range(X_AHEAD):
+            load_image(b)
+        for s in range(max(finals) + 1):
+            grouped, hidden, scored, exped = s - 1 + X_AHEAD, s - 2, s - 3, s - 4
+            finished = finals.get(s, [])
+            halves = halves_of_step(s)
+            load_image(s + X_AHEAD)
+            if s > IMAGES + 2:
+                flip_high(exped)
+                low_parts(exped)
+                flip_low(exped)
+                for half in halves:
+                    big_sums(*half)
+                    for part in range(4):
+                        small_op(*half, part)
+                for b in finished:
+                    spread_betas(b, 0)
+                    spread_betas(b, 1)
+                    scale_and_store(b, 0)
+                    scale_and_store(b, 1)
+                continue
             regroup_hidden(scored, 1)
             hidden_pass(hidden, 0)
             regroup_image(grouped, "scalar")
-            if columns:
-                open_column_sums(turn)
-            else:
-                dustbin_sums(turn)
-            sums_of(0, 2)
+            for half in halves:
+                big_sums(*half, 0)
             hidden_pass(hidden, 1)
-            sums_of(2, 4)
+            for half in halves:
+                big_sums(*half, 1)
             hidden_pass(hidden, 2)
-            sums_of(4, 6)
-            if columns:
-                sum_columns(turn)
-            else:
-                sum_rows(turn)
+            for half in halves:
+                big_sums(*half, 2)
+            for half in halves:
+                small_op(*half, 0)
             low_parts(exped)
-            if columns:
-                invert_columns(turn)
-            else:
-                invert_rows(turn)
+            for half in halves:
+                small_op(*half, 1)
             quantise_hidden(scored, 1)
-            if columns:
-                split_betas(turn, 0)
-            else:
-                split_alphas(turn, 0)
+            for half in halves:
+                small_op(*half, 2)
             hidden_pass(hidden, 3)
             cluster_scores(scored)
             regroup_image(grouped, "vector")
-            if columns:
-                split_betas(turn, 1)
-            else:
-                split_alphas(turn, 1)
+            for half in halves:
+                small_op(*half, 3)
             hidden_pass(hidden, 4)
-            flip_kernel(exped)
+            flip_high(exped)
+            flip_low(exped)
             half_tops(scored, 0)
             half_tops(scored, 1)
-            spread_betas(finished, 0)
+            for b in finished:
+                spread_betas(b, 0)
             hidden_pass(hidden, 5)
             negated_tops(scored)
             hidden_pass(hidden, 6)
-            spread_betas(finished, 1)
+            for b in finished:
+                spread_betas(b, 1)
             quantise_image(grouped)
-            scale_and_store(finished, 0)
-            scale_and_store(finished, 1)
+            for b in finished:
+                scale_and_store(b, 0)
+            for b in finished:
+                scale_and_store(b, 1)
             regroup_hidden(hidden, 0)
             quantise_hidden(hidden, 0)
             hidden_pass(hidden, 7)

@@ -23,7 +23,7 @@ CHUNKS = PIXELS // P
 CHUNKS_PER_BANK = BANK // P
 ROUNDS = 3
 RUN = 4
-SCALAR_PIXELS = 256
+SCALAR_PIXELS = 320
 STEPS_TO_ROUNDS = 5
 PAIRED = IMAGES - 2
 STREAMS = ([(b, b + 1) for b in range(0, PAIRED, 2)], [(IMAGES - 2,)], [(IMAGES - 1,)])
@@ -46,9 +46,9 @@ def tile_salad_pa_t_kernel(tc, x, Ws1, bs1, Ws2, out):
         tc.tile_pool(name="hs", bufs=2) as hs,
         tc.tile_pool(name="sk", bufs=2) as sk,
         tc.tile_pool(name="small", bufs=4) as small,
-        tc.psum_pool(name="psum_z", bufs=2) as psum_z,
+        tc.psum_pool(name="psum_z", bufs=3) as psum_z,
         tc.psum_pool(name="psum_p", bufs=2) as psum_p,
-        tc.psum_pool(name="psum_t", bufs=3) as psum_t,
+        tc.psum_pool(name="psum_t", bufs=2) as psum_t,
         tc.psum_pool(name="psum_v", bufs=1) as psum_v,
     ):
         ident = consts.tile([P, P], F32)
@@ -469,9 +469,12 @@ def tile_salad_pa_t_kernel(tc, x, Ws1, bs1, Ws2, out):
                     after = e + 1 if len(group) > 1 else 0
                     finals.setdefault(stream[2] + 2 * last_turn + after, []).append(b)
 
-        def spread_betas(b, half):
+        def spread_betas(b, half, late=False):
             number, turn, slot = last_places[b]
-            spreads[b, half] = psum_t.tile([P, CHUNKS_PER_BANK, P], F32, name="spread", tag="flip")
+            if late and half == 1:
+                spreads[b, half] = psum_p.tile([P, CHUNKS_PER_BANK, P], F32, name="late_spread", tag="score")
+            else:
+                spreads[b, half] = psum_t.tile([P, CHUNKS_PER_BANK, P], F32, name="spread", tag="flip")
             for q in range(CHUNKS_PER_BANK):
                 j = half * CHUNKS_PER_BANK + q
                 nc.tensor.transpose(
@@ -509,8 +512,8 @@ def tile_salad_pa_t_kernel(tc, x, Ws1, bs1, Ws2, out):
                     for part in range(4):
                         small_op(*half, part)
                 for b in finished:
-                    spread_betas(b, 0)
-                    spread_betas(b, 1)
+                    spread_betas(b, 0, late=True)
+                    spread_betas(b, 1, late=True)
                     scale_and_store(b, 0)
                     scale_and_store(b, 1)
                 continue

@@ -32,7 +32,6 @@ PARTS = 2
 REPEAT = 4
 ROW_WIDTH = PIXELS // P * PARTS
 KINDS = 2
-SLOT = 8
 WIDTH = REPEAT * PARTS
 
 FLOPS = 2 * IMAGES * PIXELS * (CHANNELS * HIDDEN + HIDDEN * CLUSTERS)
@@ -99,6 +98,7 @@ def tile_salad_pa_t_kernel(tc, x, Ws1, bs1, Ws2, out):
         hs_planes, hs_grouped, hs_codes, hs_scales = {}, {}, {}, {}
         scores, tops, neg_tops = {}, {}, {}
         kern, kern_lo, kern_t, first_sums = {}, {}, {}, {}
+        group_places = {}
         alphas, alpha_parts, belows, sums, betas, beta_parts, spreads, results = {}, {}, {}, {}, {}, {}, {}, {}
 
         def is_image(b):
@@ -224,7 +224,9 @@ def tile_salad_pa_t_kernel(tc, x, Ws1, bs1, Ws2, out):
             if not is_image(b):
                 return
             kern[b] = sk.tile([P, PIXELS], F32, name="kern", tag="kern", bufs=9)
-            first_sums[b] = small.tile([P, HALVES], F32, name="first_sum", tag="first_sum")
+            group, e = group_places[b]
+            if e == 0:
+                first_sums[group] = small.tile([P, len(group), HALVES], F32, name="first_sum", tag="first_sum")
             for half in range(HALVES):
                 nc.scalar.activation(
                     out=kern[b][:, half_cols(half)],
@@ -232,7 +234,7 @@ def tile_salad_pa_t_kernel(tc, x, Ws1, bs1, Ws2, out):
                     func=ACT.Exp,
                     bias=neg_tops[b][:, 0:1],
                     scale=1.0,
-                    accum_out=first_sums[b][:, half : half + 1],
+                    accum_out=first_sums[group][:, e, half : half + 1],
                 )
 
         def high_parts(b):
@@ -270,6 +272,17 @@ def tile_salad_pa_t_kernel(tc, x, Ws1, bs1, Ws2, out):
         streams = []
         for groups in STREAMS:
             streams.append((len(streams), groups, groups[0][-1] + STEPS_TO_ROUNDS))
+            for group in groups:
+                for e, b in enumerate(group):
+                    group_places[b] = (group, e)
+            for turn in range(2):
+                name = "below" + str(len(belows))
+                below = consts.tile([P, ROUNDS * len(groups[0]), KINDS], F32, name=name, tag=name)
+                nc.vector.memset(below[:], 1.0)
+                belows[len(streams) - 1, turn] = below
+
+        def below_of(stream, turn):
+            return belows[stream[0], turn % 2]
 
         def image_in_slot(stream, turn, slot):
             groups = stream[1]
@@ -392,17 +405,11 @@ def tile_salad_pa_t_kernel(tc, x, Ws1, bs1, Ws2, out):
                         )
 
         def prepare_sums(stream, turn):
-            slots = slots_of(stream, ROUNDS)
-            lo, hi = slot_range(stream, turn + 1, slots)
+            lo, hi = slot_range(stream, turn + 1, slots_of(stream, 1))
             if lo == hi:
                 return
-            below = small_tile(stream, "below", [P, slots, SLOT], F32)
-            belows[stream[0], turn] = below
-            if lo < slots_of(stream, 1):
-                nc.gpsimd.memset(below[:], 1.0)
-            for slot in range(lo, min(hi, slots_of(stream, 1))):
-                halves = first_sums[image_in_slot(stream, turn + 1, slot)]
-                nc.gpsimd.tensor_tensor(out=below[:, slot, 0:1], in0=halves[:, 0:1], in1=halves[:, 1:2], op=ALU.add)
+            group = group_places[image_in_slot(stream, turn + 1, lo)][0]
+            nc.vector.reduce_sum(out=below_of(stream, turn)[:, lo:hi, 0], in_=first_sums[group][:], axis=AX.X)
 
         def sum_rows(stream, turn):
             lo, hi = slot_range(stream, turn + 1, slots_of(stream, ROUNDS))
@@ -411,7 +418,7 @@ def tile_salad_pa_t_kernel(tc, x, Ws1, bs1, Ws2, out):
             if old >= hi:
                 return
             nc.vector.reduce_sum(
-                out=belows[stream[0], turn][:, old:hi, 0:KINDS],
+                out=below_of(stream, turn)[:, old:hi, :],
                 in_=rows_of(stream, turn, old - new, hi - new),
                 axis=AX.X,
             )
@@ -423,7 +430,7 @@ def tile_salad_pa_t_kernel(tc, x, Ws1, bs1, Ws2, out):
                 return
             alphas[stream[0], turn + 1] = small_tile(stream, "alpha", [P, slots, KINDS], F32)
             nc.vector.reciprocal(
-                out=alphas[stream[0], turn + 1][:, lo:hi, :], in_=belows[stream[0], turn][:, lo:hi, 0:KINDS]
+                out=alphas[stream[0], turn + 1][:, lo:hi, :], in_=below_of(stream, turn)[:, lo:hi, :]
             )
 
         def split_alphas(stream, turn, part):

@@ -23,7 +23,7 @@ CHUNKS = PIXELS // P
 CHUNKS_PER_BANK = BANK // P
 ROUNDS = 3
 RUN = 4
-SCALAR_PIXELS = 320
+SCALAR_PIXELS = 256
 STEPS_TO_ROUNDS = 5
 PAIRED = IMAGES - 2
 STREAMS = ([(b, b + 1) for b in range(0, PAIRED, 2)], [(IMAGES - 2,)], [(IMAGES - 1,)])

import concourse.mybir as mybir
from concourse.masks import make_identity

F32 = mybir.dt.float32
BF16 = mybir.dt.bfloat16
U32 = mybir.dt.uint32
U8 = mybir.dt.uint8
FP8X4 = mybir.dt.float8_e4m3fn_x4
ACT = mybir.ActivationFunctionType
ALU = mybir.AluOpType
AX = mybir.AxisListType

P = 128
PACK = 4
IMAGES = 16
CHANNELS = 512
HIDDEN = 512
CLUSTERS = 128
PIXELS = 1024
BANK = 512
HALVES = PIXELS // BANK
CHUNKS = PIXELS // P
CHUNKS_PER_BANK = BANK // P
ROUNDS = 3
RUN = 4
SCALAR_PIXELS = 256
STEPS_TO_ROUNDS = 5
PAIRED = IMAGES - 2
STREAMS = ([(b, b + 1) for b in range(0, PAIRED, 2)], [(IMAGES - 2,)], [(IMAGES - 1,)])
X_AHEAD = 1
PARTS = 2
REPEAT = 4
ROW_WIDTH = PIXELS // P * PARTS
KINDS = 2
WIDTH = REPEAT * PARTS

FLOPS = 2 * IMAGES * PIXELS * (CHANNELS * HIDDEN + HIDDEN * CLUSTERS)


def tile_salad_pa_t_kernel(tc, x, Ws1, bs1, Ws2, out):
    nc = tc.nc
    with (
        tc.tile_pool(name="consts", bufs=1) as consts,
        tc.tile_pool(name="xs", bufs=2) as xs,
        tc.tile_pool(name="hs", bufs=2) as hs,
        tc.tile_pool(name="sk", bufs=2) as sk,
        tc.tile_pool(name="small", bufs=4) as small,
        tc.psum_pool(name="psum_z", bufs=3) as psum_z,
        tc.psum_pool(name="psum_p", bufs=2) as psum_p,
        tc.psum_pool(name="psum_t", bufs=2) as psum_t,
        tc.psum_pool(name="psum_v", bufs=1) as psum_v,
    ):
        ident = consts.tile([P, P], F32)
        make_identity(nc, ident[:])
        ident_bf = consts.tile([P, P], BF16)
        make_identity(nc, ident_bf[:])
        pixel_mean = consts.tile([P, P], BF16)
        nc.vector.memset(pixel_mean[:], 1.0 / PIXELS)
        row_mean = consts.tile([P, P], BF16)
        nc.vector.memset(row_mean[:], 1.0 / P)

        w1_raw = consts.tile([P, PACK * CHANNELS], BF16)
        nc.sync.dma_start(out=w1_raw[:], in_=Ws1.rearrange("(p t) c -> p (t c)", t=PACK))
        w2_raw = consts.tile([P, HIDDEN], BF16)
        nc.sync.dma_start(out=w2_raw[:], in_=Ws2)
        bias_bf = consts.tile([P, PACK], BF16)
        nc.sync.dma_start(out=bias_bf[:], in_=bs1.rearrange("(p t) -> p t", t=PACK))
        bias = consts.tile([P, PACK], F32)
        nc.vector.tensor_copy(out=bias[:], in_=bias_bf[:])

        w1_grouped = consts.tile([P, PACK * P * PACK], BF16, align_bytes=64)
        w2_grouped = consts.tile([P, P * PACK], BF16, align_bytes=64)
        w1_codes = consts.tile([P, PACK * P], U32, align_bytes=64)
        w1_scales = consts.tile([P, PACK * P], U8, align_bytes=64)
        w2_codes = consts.tile([P, P], U32, align_bytes=64)
        w2_scales = consts.tile([P, P], U8, align_bytes=64)

        def group_weight_rows(rows, grouped):
            words = rows.bitcast(F32).rearrange("p (q u) -> p u q", u=2)
            flipped = psum_t.tile([P, CHUNKS_PER_BANK, P], F32, name="flipped", tag="flip")
            for u in range(2):
                nc.tensor.transpose(flipped[:, u, :], words[:, u, :], ident[:])
            nc.scalar.copy(
                out=grouped.bitcast(F32).rearrange("p (r u) -> p r u", u=2),
                in_=flipped[:, 0:2, :].rearrange("p u r -> p r u"),
            )

        for t in range(PACK):
            group_weight_rows(
                w1_raw[:, t * CHANNELS : (t + 1) * CHANNELS],
                w1_grouped[:, t * P * PACK : (t + 1) * P * PACK],
            )
        group_weight_rows(w2_raw[:], w2_grouped[:])
        nc.vector.quantize_mx(out=w1_codes[:].bitcast(FP8X4), scales=w1_scales[:], in_=w1_grouped[:])
        nc.vector.quantize_mx(out=w2_codes[:].bitcast(FP8X4), scales=w2_scales[:], in_=w2_grouped[:])

        x_raw, x_grouped, x_codes, x_scales = {}, {}, {}, {}
        hs_planes, hs_grouped, hs_codes, hs_scales = {}, {}, {}, {}
        scores, tops, neg_tops = {}, {}, {}
        kern, kern_lo, kern_t, first_sums = {}, {}, {}, {}
        group_places = {}
        alphas, alpha_parts, belows, sums, betas, beta_parts, spreads, results = {}, {}, {}, {}, {}, {}, {}, {}

        def is_image(b):
            return 0 <= b < IMAGES

        def half_cols(half):
            return slice(half * BANK, (half + 1) * BANK)

        def regrouped(dst, src):
            return (
                dst.rearrange("p (c i) j -> p c j i", i=RUN),
                src.rearrange("p j (c i) -> p c j i", i=RUN),
            )

        def load_image(b):
            if not is_image(b):
                return
            x_raw[b] = xs.tile([P, PACK, PIXELS], BF16, name="x_raw", tag="x_raw", bufs=3)
            nc.sync.dma_start(out=x_raw[b][:], in_=x[b].rearrange("(p j) h w -> p j (h w)", j=PACK))

        def regroup_image(b, engine):
            if not is_image(b):
                return
            if b not in x_grouped:
                x_grouped[b] = xs.tile([P, PIXELS, PACK], BF16, name="x_grouped", tag="x_grouped", align_bytes=64)
            cols = slice(0, SCALAR_PIXELS) if engine == "scalar" else slice(SCALAR_PIXELS, PIXELS)
            dst, src = regrouped(x_grouped[b][:, cols, :], x_raw[b][:, :, cols])
            if engine == "scalar":
                nc.scalar.copy(out=dst, in_=src)
            else:
                nc.vector.tensor_copy(out=dst, in_=src)

        def quantise_image(b):
            if not is_image(b):
                return
            x_codes[b] = xs.tile([P, PIXELS], U32, name="x_codes", tag="x_codes", bufs=2 + X_AHEAD, align_bytes=64)
            x_scales[b] = xs.tile([P, PIXELS], U8, name="x_scales", tag="x_scales", bufs=2 + X_AHEAD, align_bytes=64)
            nc.vector.quantize_mx(
                out=x_codes[b][:].bitcast(FP8X4),
                scales=x_scales[b][:],
                in_=x_grouped[b][:].rearrange("p n j -> p (n j)"),
            )

        def hidden_pass(b, k):
            if not is_image(b):
                return
            half, t = divmod(k, PACK)
            if k == 0:
                hs_planes[b] = hs.tile([P, PACK, PIXELS], BF16, name="hs_planes", tag="hs_planes")
            rows = slice(t * P, (t + 1) * P)
            z = psum_z.tile([P, BANK], F32, name="z", tag="z")
            nc.tensor.matmul_mx(
                out=z[:],
                lhsT=w1_codes[:, rows].bitcast(FP8X4),
                lhsT_scale=w1_scales[:, rows],
                rhs=x_codes[b][:, half_cols(half)].bitcast(FP8X4),
                rhs_scale=x_scales[b][:, half_cols(half)],
                start=True,
                stop=True,
            )
            nc.scalar.activation(
                out=hs_planes[b][:, t, half_cols(half)], in_=z[:], func=ACT.Relu, bias=bias[:, t : t + 1], scale=1.0
            )

        def regroup_hidden(b, half):
            if not is_image(b):
                return
            if half == 0:
                hs_grouped[b] = hs.tile([P, PIXELS, PACK], BF16, name="hs_grouped", tag="hs_grouped", align_bytes=64)
            dst, src = regrouped(hs_grouped[b][:, half_cols(half), :], hs_planes[b][:, :, half_cols(half)])
            nc.vector.tensor_copy(out=dst, in_=src)

        def quantise_hidden(b, half):
            if not is_image(b):
                return
            if half == 0:
                hs_codes[b] = hs.tile([P, PIXELS], U32, name="hs_codes", tag="hs_codes", align_bytes=64)
                hs_scales[b] = hs.tile([P, PIXELS], U8, name="hs_scales", tag="hs_scales", align_bytes=64)
            nc.vector.quantize_mx(
                out=hs_codes[b][:, half_cols(half)].bitcast(FP8X4),
                scales=hs_scales[b][:, half_cols(half)],
                in_=hs_grouped[b][:, half_cols(half), :].rearrange("p n j -> p (n j)"),
            )

        def cluster_scores(b):
            if not is_image(b):
                return
            scores[b] = []
            for half in range(HALVES):
                score = psum_p.tile([P, BANK], F32, name="score", tag="score")
                nc.tensor.matmul_mx(
                    out=score[:],
                    lhsT=w2_codes[:].bitcast(FP8X4),
                    lhsT_scale=w2_scales[:],
                    rhs=hs_codes[b][:, half_cols(half)].bitcast(FP8X4),
                    rhs_scale=hs_scales[b][:, half_cols(half)],
                    start=True,
                    stop=True,
                )
                scores[b].append(score)

        def half_tops(b, half):
            if not is_image(b):
                return
            if half == 0:
                tops[b] = small.tile([P, HALVES], F32, name="top", tag="top")
            nc.vector.reduce_max(out=tops[b][:, half : half + 1], in_=scores[b][half][:], axis=AX.X)

        def negated_tops(b):
            if not is_image(b):
                return
            neg_tops[b] = small.tile([P, 1], F32, name="neg_top", tag="neg_top")
            nc.vector.tensor_scalar(
                out=neg_tops[b][:],
                in0=tops[b][:, 0:1],
                scalar1=tops[b][:, 1:2],
                scalar2=-1.0,
                op0=ALU.max,
                op1=ALU.mult,
            )

        def exponentials(b):
            if not is_image(b):
                return
            kern[b] = sk.tile([P, PIXELS], F32, name="kern", tag="kern", bufs=9)
            group, e = group_places[b]
            if e == 0:
                first_sums[group] = small.tile([P, len(group), HALVES], F32, name="first_sum", tag="first_sum")
            for half in range(HALVES):
                nc.scalar.activation(
                    out=kern[b][:, half_cols(half)],
                    in_=scores[b][half][:],
                    func=ACT.Exp,
                    bias=neg_tops[b][:, 0:1],
                    scale=1.0,
                    accum_out=first_sums[group][:, e, half : half + 1],
                )

        def high_parts(b):
            return kern[b][:].bitcast(BF16).rearrange("p (n two) -> p two n", two=2)[:, 1, :]

        def low_parts(b):
            if not is_image(b):
                return
            kern_lo[b] = sk.tile([P, PIXELS], BF16, name="kern_lo", tag="kern_lo", bufs=8)
            nc.vector.tensor_tensor(out=kern_lo[b][:], in0=kern[b][:], in1=high_parts(b), op=ALU.subtract)

        def flip_high(b):
            if not is_image(b):
                return
            kern_t[b] = sk.tile([P, PARTS, CHUNKS, P], BF16, name="kern_t", tag="kern_t", bufs=7)
            flipped = psum_t.tile([P, CHUNKS, P], BF16, name="flipped_hi", tag="flip")
            for j in range(CHUNKS):
                nc.tensor.matmul(
                    out=flipped[:, j, :],
                    lhsT=high_parts(b)[:, j * P : (j + 1) * P],
                    rhs=ident_bf[:],
                    start=True,
                    stop=True,
                )
            nc.scalar.copy(out=kern_t[b][:, 0], in_=flipped[:])

        def flip_low(b):
            if not is_image(b):
                return
            flipped = psum_t.tile([P, CHUNKS, P], BF16, name="flipped_lo", tag="flip")
            for j in range(CHUNKS):
                nc.tensor.transpose(flipped[:, j, :], kern_lo[b][:, j * P : (j + 1) * P], ident_bf[:])
            nc.scalar.copy(out=kern_t[b][:, 1], in_=flipped[:])

        streams = []
        for groups in STREAMS:
            streams.append((len(streams), groups, groups[0][-1] + STEPS_TO_ROUNDS))
            for group in groups:
                for e, b in enumerate(group):
                    group_places[b] = (group, e)
            for turn in range(2):
                name = "below" + str(len(belows))
                below = consts.tile([P, ROUNDS * len(groups[0]), KINDS], F32, name=name, tag=name)
                nc.vector.memset(below[:], 1.0)
                belows[len(streams) - 1, turn] = below

        def below_of(stream, turn):
            return belows[stream[0], turn % 2]

        def image_in_slot(stream, turn, slot):
            groups = stream[1]
            r, e = divmod(slot, len(groups[0]))
            return groups[turn - r][e] if 0 <= turn - r < len(groups) else -1

        def slots_of(stream, rounds):
            return rounds * len(stream[1][0])

        def slot_range(stream, turn, slots):
            held = [slot for slot in range(slots) if is_image(image_in_slot(stream, turn, slot))]
            return (held[0], held[-1] + 1) if held else (0, 0)

        def small_tile(stream, name, shape, dtype):
            tag = name + str(stream[0])
            return small.tile(shape, dtype, name=tag, tag=tag)

        def split(high, low, values, part):
            if part == 0:
                nc.vector.tensor_copy(out=high, in_=values)
            else:
                nc.vector.tensor_tensor(out=low, in0=values, in1=high, op=ALU.subtract)

        def columns_of(stream, turn, lo, hi):
            end = slots_of(stream, ROUNDS) * CHUNKS * WIDTH
            return sums[stream[0], turn][:, 0:end].rearrange("p (r j c) -> p r j c", j=CHUNKS, c=WIDTH)[:, lo:hi]

        def rows_of(stream, turn, lo, hi):
            start = slots_of(stream, ROUNDS) * CHUNKS * WIDTH
            end = start + slots_of(stream, ROUNDS - 1) * KINDS * ROW_WIDTH
            return sums[stream[0], turn][:, start:end].rearrange("p (r k c) -> p r k c", k=KINDS, c=ROW_WIDTH)[:, lo:hi]

        def slots_of_piece(stream, lo, hi, piece):
            size = len(stream[1][0])
            return [slot for slot in range(lo, hi) if piece is None or slot // size == piece]

        def column_sums(stream, turn, piece):
            lo, hi = slot_range(stream, turn, slots_of(stream, ROUNDS))
            if lo == hi:
                return
            parts = alpha_parts[stream[0], turn]
            if (stream[0], turn) not in sums:
                if stream[0] == 0:
                    tile = psum_v.tile([P, BANK], F32, name="sums", tag="sums")
                else:
                    tile = psum_z.tile([P, BANK], F32, name="sums_z", tag="z")
                sums[stream[0], turn] = tile
                nc.tensor.matmul(
                    out=columns_of(stream, turn, lo, hi).rearrange("p r j c -> p r (j c)"),
                    lhsT=row_mean[:],
                    rhs=parts[:, lo:hi, 1, :].unsqueeze(2).to_broadcast([P, hi - lo, CHUNKS * REPEAT, PARTS]),
                    start=True,
                    stop=False,
                )
            for slot in slots_of_piece(stream, lo, hi, piece):
                b = image_in_slot(stream, turn, slot)
                for j in range(CHUNKS):
                    cols = slice(j * P, (j + 1) * P)
                    for part, rows in enumerate((high_parts(b), kern_lo[b][:])):
                        nc.tensor.matmul(
                            out=columns_of(stream, turn, slot, slot + 1)[:, 0, j, :],
                            lhsT=rows[:, cols],
                            rhs=parts[:, slot, 0, :].unsqueeze(1).to_broadcast([P, REPEAT, PARTS]),
                            start=False,
                            stop=(slot == hi - 1 and j == CHUNKS - 1 and part == PARTS - 1),
                        )

        def sum_columns(stream, turn):
            slots = slots_of(stream, ROUNDS)
            lo, hi = slot_range(stream, turn, slots)
            if lo == hi:
                return
            betas[stream[0], turn] = small_tile(stream, "beta", [P, slots, CHUNKS], F32)
            nc.vector.reduce_sum(
                out=betas[stream[0], turn][:, lo:hi, :],
                in_=columns_of(stream, turn, lo, hi)[:, :, :, 0:PARTS],
                axis=AX.X,
            )

        def invert_columns(stream, turn):
            lo, hi = slot_range(stream, turn, slots_of(stream, ROUNDS))
            if lo == hi:
                return
            beta = betas[stream[0], turn][:, lo:hi, :]
            nc.vector.reciprocal(out=beta, in_=beta)

        def split_betas(stream, turn, part):
            slots = slots_of(stream, ROUNDS - 1)
            lo, hi = slot_range(stream, turn, slots)
            if lo == hi:
                return
            if part == 0:
                beta_parts[stream[0], turn] = small_tile(stream, "beta_part", [P, slots, CHUNKS, PARTS], BF16)
            parts = beta_parts[stream[0], turn][:, lo:hi]
            split(parts[:, :, :, 0], parts[:, :, :, 1], betas[stream[0], turn][:, lo:hi, :], part)

        def row_sums(stream, turn, piece):
            lo, hi = slot_range(stream, turn, slots_of(stream, ROUNDS - 1))
            if lo == hi:
                return
            parts = beta_parts[stream[0], turn]
            if not piece:
                nc.tensor.matmul(
                    out=rows_of(stream, turn, lo, hi)[:, :, 1, :],
                    lhsT=pixel_mean[:],
                    rhs=parts[:, lo:hi].rearrange("p r j c -> p r (j c)"),
                    start=True,
                    stop=True,
                )
            for slot in slots_of_piece(stream, lo, hi, piece):
                b = image_in_slot(stream, turn, slot)
                for j in range(CHUNKS):
                    for part in range(PARTS):
                        nc.tensor.matmul(
                            out=rows_of(stream, turn, slot, slot + 1)[:, 0, 0, j * PARTS : (j + 1) * PARTS],
                            lhsT=kern_t[b][:, part, j, :],
                            rhs=parts[:, slot, j, :],
                            start=(part == 0),
                            stop=(part == PARTS - 1),
                        )

        def prepare_sums(stream, turn):
            lo, hi = slot_range(stream, turn + 1, slots_of(stream, 1))
            if lo == hi:
                return
            group = group_places[image_in_slot(stream, turn + 1, lo)][0]
            nc.vector.reduce_sum(out=below_of(stream, turn)[:, lo:hi, 0], in_=first_sums[group][:], axis=AX.X)

        def sum_rows(stream, turn):
            lo, hi = slot_range(stream, turn + 1, slots_of(stream, ROUNDS))
            new = slots_of(stream, 1)
            old = max(lo, new)
            if old >= hi:
                return
            nc.vector.reduce_sum(
                out=below_of(stream, turn)[:, old:hi, :],
                in_=rows_of(stream, turn, old - new, hi - new),
                axis=AX.X,
            )

        def invert_rows(stream, turn):
            slots = slots_of(stream, ROUNDS)
            lo, hi = slot_range(stream, turn + 1, slots)
            if lo == hi:
                return
            alphas[stream[0], turn + 1] = small_tile(stream, "alpha", [P, slots, KINDS], F32)
            nc.vector.reciprocal(
                out=alphas[stream[0], turn + 1][:, lo:hi, :], in_=below_of(stream, turn)[:, lo:hi, :]
            )

        def split_alphas(stream, turn, part):
            slots = slots_of(stream, ROUNDS)
            lo, hi = slot_range(stream, turn + 1, slots)
            if lo == hi:
                return
            if part == 0:
                alpha_parts[stream[0], turn + 1] = small_tile(stream, "alpha_part", [P, slots, KINDS, PARTS], BF16)
            parts = alpha_parts[stream[0], turn + 1][:, lo:hi]
            split(parts[:, :, :, 0], parts[:, :, :, 1], alphas[stream[0], turn + 1][:, lo:hi, :], part)

        def halves_of_step(s):
            found = []
            for stream in reversed(streams):
                turn, kind = divmod(s - stream[2], 2)
                found.append((stream, turn, kind))
            return found

        def big_sums(stream, turn, kind, piece=None):
            if kind == 0:
                column_sums(stream, turn, piece)
            else:
                if not piece:
                    prepare_sums(stream, turn)
                row_sums(stream, turn, piece)

        def small_op(stream, turn, kind, part):
            if part == 0:
                (sum_columns, sum_rows)[kind](stream, turn)
            elif part == 1:
                (invert_columns, invert_rows)[kind](stream, turn)
            else:
                (split_betas, split_alphas)[kind](stream, turn, part - 2)

        last_places = {}
        finals = {}
        for stream in streams:
            for g, group in enumerate(stream[1]):
                for e, b in enumerate(group):
                    last_turn = g + ROUNDS - 1
                    last_places[b] = (stream[0], last_turn, (ROUNDS - 1) * len(group) + e)
                    after = e + 1 if len(group) > 1 else 0
                    finals.setdefault(stream[2] + 2 * last_turn + after, []).append(b)

        def spread_betas(b, half, late=False):
            number, turn, slot = last_places[b]
            if late and half == 1:
                spreads[b, half] = psum_p.tile([P, CHUNKS_PER_BANK, P], F32, name="late_spread", tag="score")
            else:
                spreads[b, half] = psum_t.tile([P, CHUNKS_PER_BANK, P], F32, name="spread", tag="flip")
            for q in range(CHUNKS_PER_BANK):
                j = half * CHUNKS_PER_BANK + q
                nc.tensor.transpose(
                    spreads[b, half][:, q, :], betas[number, turn][:, slot, j : j + 1].to_broadcast([P, P]), ident[:]
                )

        def scale_and_store(b, half):
            number, turn, slot = last_places[b]
            if half == 0:
                results[b] = sk.tile([P, PIXELS], F32, name="result", tag="result", bufs=4)
            cols = half_cols(half)
            nc.vector.scalar_tensor_tensor(
                out=results[b][:, cols],
                in0=kern[b][:, cols],
                scalar=alphas[number, turn][:, slot, 0:1],
                in1=spreads[b, half][:].rearrange("p q n -> p (q n)"),
                op0=ALU.mult,
                op1=ALU.mult,
            )
            nc.sync.dma_start(out=out[b][:, cols], in_=results[b][:, cols])

        for b in range(X_AHEAD):
            load_image(b)
        for s in range(max(finals) + 1):
            grouped, hidden, scored, exped = s - 1 + X_AHEAD, s - 2, s - 3, s - 4
            finished = finals.get(s, [])
            halves = halves_of_step(s)
            load_image(s + X_AHEAD)
            if s > IMAGES + 2:
                flip_high(exped)
                low_parts(exped)
                flip_low(exped)
                for half in halves:
                    big_sums(*half)
                    for part in range(4):
                        small_op(*half, part)
                for b in finished:
                    spread_betas(b, 0, late=True)
                    spread_betas(b, 1, late=True)
                    scale_and_store(b, 0)
                    scale_and_store(b, 1)
                continue
            regroup_hidden(scored, 1)
            hidden_pass(hidden, 0)
            regroup_image(grouped, "scalar")
            for half in halves:
                big_sums(*half, 0)
            hidden_pass(hidden, 1)
            for half in halves:
                big_sums(*half, 1)
            hidden_pass(hidden, 2)
            for half in halves:
                big_sums(*half, 2)
            for half in halves:
                small_op(*half, 0)
            low_parts(exped)
            for half in halves:
                small_op(*half, 1)
            quantise_hidden(scored, 1)
            for half in halves:
                small_op(*half, 2)
            hidden_pass(hidden, 3)
            cluster_scores(scored)
            regroup_image(grouped, "vector")
            for half in halves:
                small_op(*half, 3)
            hidden_pass(hidden, 4)
            flip_high(exped)
            flip_low(exped)
            half_tops(scored, 0)
            half_tops(scored, 1)
            for b in finished:
                spread_betas(b, 0)
            hidden_pass(hidden, 5)
            negated_tops(scored)
            hidden_pass(hidden, 6)
            for b in finished:
                spread_betas(b, 1)
            quantise_image(grouped)
            for b in finished:
                scale_and_store(b, 0)
            for b in finished:
                scale_and_store(b, 1)
            regroup_hidden(hidden, 0)
            quantise_hidden(hidden, 0)
            hidden_pass(hidden, 7)
            exponentials(scored)
